import numpy as np
import ml_dtypes


def mxq(x, axis, fmt="e4m3"):
    dtype, down = {"e4m3": (ml_dtypes.float8_e4m3fn, 7), "e5m2": (ml_dtypes.float8_e5m2, 14)}[fmt]
    v = np.moveaxis(np.asarray(x, np.float32).astype(ml_dtypes.bfloat16).astype(np.float64), axis, -1)
    blocks = v.reshape(v.shape[:-1] + (-1, 32))
    amax = np.abs(blocks).max(-1, keepdims=True)
    byte = np.maximum(np.where(amax > 0, np.frexp(amax)[1] - 1 + 127, 0) - down, 1)
    scale = np.exp2(byte - 127.0)
    codes = (blocks / scale).astype(np.float32).astype(dtype).astype(np.float64)
    return np.moveaxis((codes * scale).reshape(v.shape), -1, axis)


WIDE = False


def mx_kscale(k):
    if not WIDE:
        return np.ones(k)
    levels = np.array([10, -10, 5, -5, 0])
    if k % 512:
        return np.exp2(np.random.permutation(np.resize(levels, k // 32))).repeat(32)
    a = np.empty((k // 512, 16))
    for p in range(k // 512):
        a[p, :8] = np.random.permutation(np.resize(levels, 8))
        for g in range(8):
            far = levels[np.abs(levels - a[p, g]) >= 10]
            a[p, g + 8] = far[np.random.randint(len(far))]
    return np.exp2(a.ravel()).repeat(32)


BF16 = ml_dtypes.bfloat16


def bf(x):
    return np.asarray(x, np.float32).astype(BF16)


def f64(x):
    return np.asarray(x).astype(np.float64)


B, IN, HID, PROJ, H, KC = 8192, 512, 128, 128, 4, 4
EPS = 1e-5


def silu(v):
    return v / (1.0 + np.exp(-v))


def layernorm(v, w, b):
    mu = v.mean(-1, keepdims=True)
    var = ((v - mu) ** 2).mean(-1, keepdims=True)
    return (v - mu) / np.sqrt(var + EPS) * w + b


def causal_conv(v, w, b):
    vp = np.pad(v, ((0, 0), (KC - 1, 0)))
    L = v.shape[1]
    return b + sum(w[j] * vp[:, j:j + L] for j in range(KC))


def setup_inputs():
    s = mx_kscale(IN)
    r = np.random.standard_normal
    return {"x": bf(r((B, IN))),
            "ln_w": bf((1.0 + 0.1 * r(IN)) * s), "ln_b": bf(0.1 * r(IN) * s),
            "upL_w": bf(r((IN, PROJ)) / np.sqrt(IN) / s[:, None]), "upL_b": bf(0.2 * r(PROJ)),
            "upR_w": bf(r((IN, HID)) / np.sqrt(IN) / s[:, None]), "upR_b": bf(0.2 * r(HID)),
            "conv_w": bf((1.0 + 0.3 * r(KC)) / np.sqrt(KC)), "conv_b": bf(0.2 + 0.1 * r(1))}


def reference(x, ln_w, ln_b, upL_w, upL_b, upR_w, upR_b, conv_w, conv_b):
    xn = mxq(layernorm(f64(x), f64(ln_w), f64(ln_b)), 1, "e4m3")
    x_left = (xn @ mxq(f64(upL_w), 0, "e4m3")) + f64(upL_b)
    x_right = (xn @ mxq(f64(upR_w), 0, "e4m3")) + f64(upR_b)
    x_conv = silu(causal_conv(x_left, f64(conv_w), f64(conv_b)))
    return x_left, x_conv, x_right

@@ -1,0 +1,330 @@
+from contextlib import ExitStack
+
+import concourse.mybir as mybir
+from concourse.masks import make_identity
+
+F32 = mybir.dt.float32
+BF16 = mybir.dt.bfloat16
+U32 = mybir.dt.uint32
+U8 = mybir.dt.uint8
+FP8X4 = mybir.dt.float8_e4m3fn_x4
+ALU = mybir.AluOpType
+ACT = mybir.ActivationFunctionType
+
+P = 128
+PACK = 4
+ROWS, IN, FEAT, TAPS = 8192, 512, 128, 4
+EPS = 1e-5
+SUB = 4
+GROUP_ROWS = P * SUB
+N_GROUPS = ROWS // GROUP_ROWS
+SUB_ON_TENSOR = 3
+BANKS_ON_SCALAR = 3
+
+FLOPS = 2 * ROWS * IN * 2 * FEAT
+
+
+def tile_mlstmblock_pa_t_kernel(
+    tc, x, ln_w, ln_b, upL_w, upL_b, upR_w, upR_b, conv_w, conv_b, out_0, out_1, out_2
+):
+    nc = tc.nc
+    with ExitStack() as ctx:
+        const = ctx.enter_context(tc.tile_pool(name="const", bufs=1))
+        xin = ctx.enter_context(tc.tile_pool(name="xin", bufs=1))
+        small = ctx.enter_context(tc.tile_pool(name="small", bufs=4))
+        work = ctx.enter_context(tc.tile_pool(name="work", bufs=3))
+        tpsum = ctx.enter_context(tc.psum_pool(name="tpsum", bufs=1))
+        mpsum = ctx.enter_context(tc.psum_pool(name="mpsum", bufs=2))
+
+        def group_rows(dram, g):
+            return dram[g * GROUP_ROWS : (g + 1) * GROUP_ROWS, :].rearrange(
+                "(p j) n -> p j n", j=SUB
+            )
+
+        x_sb = [xin.tile([P, SUB, IN], BF16, name="x%d" % g) for g in range(N_GROUPS)]
+        for g in range(N_GROUPS):
+            nc.sync.dma_start(out=x_sb[g][:], in_=group_rows(x, g))
+        lnw_bf = const.tile([P, PACK], BF16, name="lnw_bf")
+        nc.scalar.dma_start(out=lnw_bf[:], in_=ln_w.rearrange("(p c) -> p c", c=PACK))
+        lnb_bf = const.tile([P, PACK], BF16, name="lnb_bf")
+        nc.scalar.dma_start(out=lnb_bf[:], in_=ln_b.rearrange("(p c) -> p c", c=PACK))
+        lbias_bf = const.tile([P, 1], BF16, name="lbias_bf")
+        nc.scalar.dma_start(out=lbias_bf[:], in_=upL_b.rearrange("(p c) -> p c", c=1))
+        w_raw = const.tile([P, PACK, 2 * FEAT], BF16, name="w_raw")
+        nc.scalar.dma_start(
+            out=w_raw[:, :, 0:FEAT], in_=upL_w.rearrange("(p c) n -> p c n", c=PACK)
+        )
+        nc.scalar.dma_start(
+            out=w_raw[:, :, FEAT : 2 * FEAT], in_=upR_w.rearrange("(p c) n -> p c n", c=PACK)
+        )
+        bias_bf = const.tile([P, 2 * FEAT], BF16, name="bias_bf")
+        nc.scalar.dma_start(out=bias_bf[:, 0:FEAT], in_=upL_b.partition_broadcast(P))
+        nc.scalar.dma_start(out=bias_bf[:, FEAT : 2 * FEAT], in_=upR_b.partition_broadcast(P))
+        taps_bf = const.tile([P, TAPS], BF16, name="taps_bf")
+        nc.scalar.dma_start(out=taps_bf[:], in_=conv_w.partition_broadcast(P))
+        cbias_bf = const.tile([P, 1], BF16, name="cbias_bf")
+        nc.scalar.dma_start(out=cbias_bf[:], in_=conv_b.partition_broadcast(P))
+
+        ident = const.tile([P, P], F32, name="ident")
+        make_identity(nc, ident[:])
+        neg_half = const.tile([P, SUB], F32, name="neg_half")
+        nc.gpsimd.memset(neg_half[:], -0.5)
+
+        mean_var = {}
+        normed = {}
+        t_banks = {}
+        planes_of = {}
+        grouped = {}
+        mx_words = {}
+        row_banks = {}
+        left_t_bank = {}
+        left_t = {}
+        conv_bank = {}
+        conv_last = {}
+
+        def stats(g):
+            st = small.tile([P, SUB, 6], F32, name="st")
+            mv = small.tile([P, SUB, 2], F32, name="mv")
+            for j in range(SUB):
+                nc.vector.bn_stats(out=st[:, j, :], in_=x_sb[g][:, j, :])
+            for j in range(SUB):
+                nc.vector.bn_aggr(out=mv[:, j, :], in_=st[:, j, :])
+            var_eps = small.tile([P, SUB], F32, name="var_eps")
+            nc.vector.tensor_scalar(
+                out=var_eps[:], in0=mv[:, :, 1], scalar1=EPS, scalar2=None, op0=ALU.add
+            )
+            neg_mean = small.tile([P, SUB], F32, name="neg_mean")
+            nc.vector.tensor_scalar(
+                out=neg_mean[:], in0=mv[:, :, 0], scalar1=-1.0, scalar2=None, op0=ALU.mult
+            )
+            mean_var[g] = (neg_mean, var_eps)
+
+        def constants():
+            cols = const.tile([P, 2 * PACK + 1], F32, name="cols")
+            nc.vector.tensor_copy(out=cols[:, 0:PACK], in_=lnw_bf[:])
+            nc.vector.tensor_copy(out=cols[:, PACK : 2 * PACK], in_=lnb_bf[:])
+            nc.vector.tensor_copy(out=cols[:, 2 * PACK : 2 * PACK + 1], in_=lbias_bf[:])
+            w_grouped = const.tile([P, 2 * FEAT, PACK], BF16, name="w_grouped", align_bytes=64)
+            nc.vector.tensor_copy(out=w_grouped[:], in_=w_raw[:].rearrange("p c n -> p n c"))
+            w_codes = const.tile([P, 2 * FEAT], U32, name="w_codes", align_bytes=64)
+            w_scales = const.tile([P, 2 * FEAT], U8, name="w_scales", align_bytes=64)
+            bias_bc = const.tile([P, 2 * FEAT], F32, name="bias_bc")
+            nc.vector.tensor_copy(out=bias_bc[:], in_=bias_bf[:])
+            nc.vector.quantize_mx(
+                out=w_codes[:].bitcast(FP8X4),
+                scales=w_scales[:],
+                in_=w_grouped[:].rearrange("p n c -> p (n c)"),
+            )
+            taps = const.tile([P, TAPS], F32, name="taps")
+            nc.vector.tensor_copy(out=taps[:], in_=taps_bf[:])
+            cbias = const.tile([P, 1], F32, name="cbias")
+            nc.vector.tensor_copy(out=cbias[:], in_=cbias_bf[:])
+            band = const.tile([P, FEAT], F32, name="band")
+            nc.vector.tensor_scalar(
+                out=band[:], in0=ident[:], scalar1=taps[:, TAPS - 1 : TAPS], scalar2=None, op0=ALU.mult
+            )
+            for s in range(1, TAPS):
+                nc.vector.scalar_tensor_tensor(
+                    out=band[:, s:FEAT],
+                    in0=ident[:, 0 : FEAT - s],
+                    scalar=taps[:, TAPS - 1 - s : TAPS - s],
+                    in1=band[:, s:FEAT],
+                    op0=ALU.mult,
+                    op1=ALU.add,
+                )
+            conv_of_bias = const.tile([P, FEAT], F32, name="conv_of_bias")
+            nc.vector.tensor_scalar(
+                out=conv_of_bias[:],
+                in0=bias_bc[:, 0:FEAT],
+                scalar1=taps[:, TAPS - 1 : TAPS],
+                scalar2=cbias[:, 0:1],
+                op0=ALU.mult,
+                op1=ALU.add,
+            )
+            for s in range(1, TAPS):
+                nc.vector.scalar_tensor_tensor(
+                    out=conv_of_bias[:, s:FEAT],
+                    in0=bias_bc[:, 0 : FEAT - s],
+                    scalar=taps[:, TAPS - 1 - s : TAPS - s],
+                    in1=conv_of_bias[:, s:FEAT],
+                    op0=ALU.mult,
+                    op1=ALU.add,
+                )
+            return cols, w_codes, w_scales, bias_bc, taps, cbias, band, conv_of_bias
+
+        def normalise(g):
+            neg_mean, var_eps = mean_var.pop(g)
+            rstd = small.tile([P, SUB], F32, name="rstd")
+            nc.gpsimd.tensor_tensor(out=rstd[:], in0=var_eps[:], in1=neg_half[:], op=ALU.pow)
+            t = work.tile([P, SUB, IN], F32, name="t")
+            for j in range(SUB):
+                nc.gpsimd.tensor_scalar(
+                    out=t[:, j, :].rearrange("p (c m) -> p c m", c=PACK),
+                    in0=x_sb[g][:, j, :].rearrange("p (m c) -> p c m", c=PACK),
+                    scalar1=neg_mean[:, j : j + 1],
+                    scalar2=rstd[:, j : j + 1],
+                    op0=ALU.add,
+                    op1=ALU.mult,
+                )
+            normed[g] = t
+
+        def transpose(g):
+            t = normed.pop(g)
+            banks = [
+                tpsum.tile([P, GROUP_ROWS], F32, name="bank", tag="tp%d" % c) for c in range(PACK)
+            ]
+            for c in range(PACK):
+                for j in range(SUB):
+                    nc.tensor.transpose(
+                        out=banks[c][:, j * P : (j + 1) * P],
+                        in_=t[:, j, c * P : (c + 1) * P],
+                        identity=ident[:],
+                    )
+            t_banks[g] = banks
+
+        def scale_shift(g):
+            banks = t_banks.pop(g)
+            planes = work.tile([P, PACK, GROUP_ROWS], BF16, name="planes")
+            for c in range(BANKS_ON_SCALAR, PACK):
+                nc.vector.tensor_scalar(
+                    out=planes[:, c, :],
+                    in0=banks[c][:],
+                    scalar1=cols[:, c : c + 1],
+                    scalar2=cols[:, PACK + c : PACK + c + 1],
+                    op0=ALU.mult,
+                    op1=ALU.add,
+                )
+            for c in range(BANKS_ON_SCALAR):
+                nc.scalar.activation(
+                    out=planes[:, c, :],
+                    in_=banks[c][:],
+                    func=ACT.Identity,
+                    scale=cols[:, c : c + 1],
+                    bias=cols[:, PACK + c : PACK + c + 1],
+                )
+            planes_of[g] = planes
+
+        def regroup(g):
+            planes = planes_of.pop(g)
+            grp = work.tile([P, GROUP_ROWS, PACK], BF16, name="grp", align_bytes=64)
+            nc.scalar.copy(
+                out=grp[:].rearrange("p (q i) c -> p q c i", i=4),
+                in_=planes[:].rearrange("p c (q i) -> p q c i", i=4),
+            )
+            grouped[g] = grp
+
+        def quantise(g):
+            grp = grouped.pop(g)
+            codes = work.tile([P, GROUP_ROWS], U32, name="codes", align_bytes=64)
+            scales = work.tile([P, GROUP_ROWS], U8, name="scales", align_bytes=64)
+            nc.vector.quantize_mx(
+                out=codes[:].bitcast(FP8X4),
+                scales=scales[:],
+                in_=grp[:].rearrange("p r c -> p (r c)"),
+            )
+            mx_words[g] = (codes, scales)
+
+        def project(g):
+            codes, scales = mx_words.pop(g)
+            banks = []
+            for h in range(SUB // 2):
+                acc = mpsum.tile([P, 2, 2 * FEAT], F32, name="acc")
+                for i in range(2):
+                    sub_cols = slice((2 * h + i) * P, (2 * h + i + 1) * P)
+                    nc.tensor.matmul_mx(
+                        out=acc[:, i, :],
+                        lhsT=codes[:, sub_cols].bitcast(FP8X4),
+                        lhsT_scale=scales[:, sub_cols],
+                        rhs=w_codes[:].bitcast(FP8X4),
+                        rhs_scale=w_scales[:],
+                        start=True,
+                        stop=True,
+                    )
+                banks.append(acc)
+            row_banks[g] = banks
+            lt = tpsum.tile([P, GROUP_ROWS], F32, name="lt")
+            nc.tensor.matmul_mx(
+                out=lt[:],
+                lhsT=w_codes[:, 0:FEAT].bitcast(FP8X4),
+                lhsT_scale=w_scales[:, 0:FEAT],
+                rhs=codes[:].bitcast(FP8X4),
+                rhs_scale=scales[:],
+                start=True,
+                stop=True,
+            )
+            left_t_bank[g] = lt
+
+        def left_bias(g):
+            lt = left_t_bank.pop(g)
+            xlt = work.tile([P, GROUP_ROWS], F32, name="xlt")
+            nc.scalar.activation(
+                out=xlt[:], in_=lt[:], func=ACT.Identity, bias=cols[:, 2 * PACK : 2 * PACK + 1]
+            )
+            left_t[g] = xlt
+
+        def convolve_on_tensor(g):
+            xlt = left_t.pop(g)
+            cvp = tpsum.tile([P, SUB_ON_TENSOR, FEAT], F32, name="cvp")
+            for j in range(SUB_ON_TENSOR):
+                nc.tensor.matmul(
+                    out=cvp[:, j, :],
+                    lhsT=xlt[:, j * P : (j + 1) * P],
+                    rhs=band[:],
+                    start=True,
+                    stop=True,
+                )
+            conv_bank[g] = cvp
+
+        def add_bias_and_convolve_last(g):
+            banks = row_banks.pop(g)
+            o = work.tile([P, 2, SUB, FEAT], F32, name="o")
+            cv = work.tile([P, FEAT], F32, name="cv")
+            last_left = banks[SUB // 2 - 1][:, 1, 0:FEAT]
+            for s in range(TAPS):
+                nc.vector.scalar_tensor_tensor(
+                    out=cv[:, s:FEAT],
+                    in0=last_left[:, 0 : FEAT - s],
+                    scalar=taps[:, TAPS - 1 - s : TAPS - s],
+                    in1=conv_of_bias[:] if s == 0 else cv[:, s:FEAT],
+                    op0=ALU.mult,
+                    op1=ALU.add,
+                )
+                if s < SUB // 2:
+                    nc.vector.tensor_tensor(
+                        out=o[:, :, 2 * s : 2 * s + 2, :].rearrange("p l j n -> p j l n"),
+                        in0=banks[s][:].rearrange("p j (l n) -> p j l n", l=2),
+                        in1=bias_bc[:]
+                        .rearrange("p (l n) -> p l n", l=2)
+                        .unsqueeze(1)
+                        .to_broadcast([P, 2, 2, FEAT]),
+                        op=ALU.add,
+                    )
+            nc.sync.dma_start(out=group_rows(out_0, g), in_=o[:, 0, :, :])
+            nc.sync.dma_start(out=group_rows(out_2, g), in_=o[:, 1, :, :])
+            conv_last[g] = cv
+
+        def silu(g):
+            cvp = conv_bank.pop(g)
+            cv = conv_last.pop(g)
+            xc = work.tile([P, SUB, FEAT], F32, name="xc")
+            nc.scalar.activation(
+                out=xc[:, 0:SUB_ON_TENSOR, :], in_=cvp[:], func=ACT.Silu, bias=cbias[:, 0:1]
+            )
+            nc.scalar.activation(out=xc[:, SUB_ON_TENSOR, :], in_=cv[:], func=ACT.Silu)
+            nc.sync.dma_start(out=group_rows(out_1, g), in_=xc[:])
+
+        stats(0)
+        cols, w_codes, w_scales, bias_bc, taps, cbias, band, conv_of_bias = constants()
+        for g in range(N_GROUPS):
+            if g > 0:
+                stats(g)
+            normalise(g)
+            transpose(g)
+            scale_shift(g)
+            regroup(g)
+            quantise(g)
+            project(g)
+            left_bias(g)
+            convolve_on_tensor(g)
+            add_bias_and_convolve_last(g)
+            silu(g)

@@ -19,7 +19,7 @@ SUB = 4
 GROUP_ROWS = P * SUB
 N_GROUPS = ROWS // GROUP_ROWS
 SUB_ON_TENSOR = 3
-BANKS_ON_SCALAR = 3
+ROWS_ON_SCALAR = 256
 
 FLOPS = 2 * ROWS * IN * 2 * FEAT
 
@@ -34,7 +34,7 @@ def tile_mlstmblock_pa_t_kernel(
         small = ctx.enter_context(tc.tile_pool(name="small", bufs=4))
         work = ctx.enter_context(tc.tile_pool(name="work", bufs=3))
         tpsum = ctx.enter_context(tc.psum_pool(name="tpsum", bufs=1))
-        mpsum = ctx.enter_context(tc.psum_pool(name="mpsum", bufs=2))
+        mpsum = ctx.enter_context(tc.psum_pool(name="mpsum", bufs=1))
 
         def group_rows(dram, g):
             return dram[g * GROUP_ROWS : (g + 1) * GROUP_ROWS, :].rearrange(
@@ -57,9 +57,8 @@ def tile_mlstmblock_pa_t_kernel(
         nc.scalar.dma_start(
             out=w_raw[:, :, FEAT : 2 * FEAT], in_=upR_w.rearrange("(p c) n -> p c n", c=PACK)
         )
-        bias_bf = const.tile([P, 2 * FEAT], BF16, name="bias_bf")
-        nc.scalar.dma_start(out=bias_bf[:, 0:FEAT], in_=upL_b.partition_broadcast(P))
-        nc.scalar.dma_start(out=bias_bf[:, FEAT : 2 * FEAT], in_=upR_b.partition_broadcast(P))
+        bias_bf = const.tile([P, FEAT], BF16, name="bias_bf")
+        nc.scalar.dma_start(out=bias_bf[:], in_=upR_b.partition_broadcast(P))
         taps_bf = const.tile([P, TAPS], BF16, name="taps_bf")
         nc.scalar.dma_start(out=taps_bf[:], in_=conv_w.partition_broadcast(P))
         cbias_bf = const.tile([P, 1], BF16, name="cbias_bf")
@@ -76,7 +75,8 @@ def tile_mlstmblock_pa_t_kernel(
         planes_of = {}
         grouped = {}
         mx_words = {}
-        row_banks = {}
+        right_bank = {}
+        left_bank = {}
         left_t_bank = {}
         left_t = {}
         conv_bank = {}
@@ -108,7 +108,7 @@ def tile_mlstmblock_pa_t_kernel(
             nc.vector.tensor_copy(out=w_grouped[:], in_=w_raw[:].rearrange("p c n -> p n c"))
             w_codes = const.tile([P, 2 * FEAT], U32, name="w_codes", align_bytes=64)
             w_scales = const.tile([P, 2 * FEAT], U8, name="w_scales", align_bytes=64)
-            bias_bc = const.tile([P, 2 * FEAT], F32, name="bias_bc")
+            bias_bc = const.tile([P, FEAT], F32, name="bias_bc")
             nc.vector.tensor_copy(out=bias_bc[:], in_=bias_bf[:])
             nc.vector.quantize_mx(
                 out=w_codes[:].bitcast(FP8X4),
@@ -132,25 +132,7 @@ def tile_mlstmblock_pa_t_kernel(
                     op0=ALU.mult,
                     op1=ALU.add,
                 )
-            conv_of_bias = const.tile([P, FEAT], F32, name="conv_of_bias")
-            nc.vector.tensor_scalar(
-                out=conv_of_bias[:],
-                in0=bias_bc[:, 0:FEAT],
-                scalar1=taps[:, TAPS - 1 : TAPS],
-                scalar2=cbias[:, 0:1],
-                op0=ALU.mult,
-                op1=ALU.add,
-            )
-            for s in range(1, TAPS):
-                nc.vector.scalar_tensor_tensor(
-                    out=conv_of_bias[:, s:FEAT],
-                    in0=bias_bc[:, 0 : FEAT - s],
-                    scalar=taps[:, TAPS - 1 - s : TAPS - s],
-                    in1=conv_of_bias[:, s:FEAT],
-                    op0=ALU.mult,
-                    op1=ALU.add,
-                )
-            return cols, w_codes, w_scales, bias_bc, taps, cbias, band, conv_of_bias
+            return cols, w_codes, w_scales, bias_bc, taps, cbias, band
 
         def normalise(g):
             neg_mean, var_eps = mean_var.pop(g)
@@ -185,16 +167,7 @@ def tile_mlstmblock_pa_t_kernel(
         def scale_shift(g):
             banks = t_banks.pop(g)
             planes = work.tile([P, PACK, GROUP_ROWS], BF16, name="planes")
-            for c in range(BANKS_ON_SCALAR, PACK):
-                nc.vector.tensor_scalar(
-                    out=planes[:, c, :],
-                    in0=banks[c][:],
-                    scalar1=cols[:, c : c + 1],
-                    scalar2=cols[:, PACK + c : PACK + c + 1],
-                    op0=ALU.mult,
-                    op1=ALU.add,
-                )
-            for c in range(BANKS_ON_SCALAR):
+            for c in range(PACK):
                 nc.scalar.activation(
                     out=planes[:, c, :],
                     in_=banks[c][:],
@@ -207,9 +180,17 @@ def tile_mlstmblock_pa_t_kernel(
         def regroup(g):
             planes = planes_of.pop(g)
             grp = work.tile([P, GROUP_ROWS, PACK], BF16, name="grp", align_bytes=64)
+            nc.gpsimd.tensor_scalar(
+                out=grp[:, ROWS_ON_SCALAR:, :],
+                in0=planes[:, :, ROWS_ON_SCALAR:].rearrange("p c r -> p r c"),
+                scalar1=1.0,
+                scalar2=0.0,
+                op0=ALU.mult,
+                op1=ALU.add,
+            )
             nc.scalar.copy(
-                out=grp[:].rearrange("p (q i) c -> p q c i", i=4),
-                in_=planes[:].rearrange("p c (q i) -> p q c i", i=4),
+                out=grp[:, 0:ROWS_ON_SCALAR, :].rearrange("p (q i) c -> p q c i", i=4),
+                in_=planes[:, :, 0:ROWS_ON_SCALAR].rearrange("p c (q i) -> p q c i", i=4),
             )
             grouped[g] = grp
 
@@ -226,22 +207,6 @@ def tile_mlstmblock_pa_t_kernel(
 
         def project(g):
             codes, scales = mx_words.pop(g)
-            banks = []
-            for h in range(SUB // 2):
-                acc = mpsum.tile([P, 2, 2 * FEAT], F32, name="acc")
-                for i in range(2):
-                    sub_cols = slice((2 * h + i) * P, (2 * h + i + 1) * P)
-                    nc.tensor.matmul_mx(
-                        out=acc[:, i, :],
-                        lhsT=codes[:, sub_cols].bitcast(FP8X4),
-                        lhsT_scale=scales[:, sub_cols],
-                        rhs=w_codes[:].bitcast(FP8X4),
-                        rhs_scale=w_scales[:],
-                        start=True,
-                        stop=True,
-                    )
-                banks.append(acc)
-            row_banks[g] = banks
             lt = tpsum.tile([P, GROUP_ROWS], F32, name="lt")
             nc.tensor.matmul_mx(
                 out=lt[:],
@@ -253,6 +218,19 @@ def tile_mlstmblock_pa_t_kernel(
                 stop=True,
             )
             left_t_bank[g] = lt
+            right = mpsum.tile([P, SUB, FEAT], F32, name="right")
+            for j in range(SUB):
+                sub_cols = slice(j * P, (j + 1) * P)
+                nc.tensor.matmul_mx(
+                    out=right[:, j, :],
+                    lhsT=codes[:, sub_cols].bitcast(FP8X4),
+                    lhsT_scale=scales[:, sub_cols],
+                    rhs=w_codes[:, FEAT : 2 * FEAT].bitcast(FP8X4),
+                    rhs_scale=w_scales[:, FEAT : 2 * FEAT],
+                    start=True,
+                    stop=True,
+                )
+            right_bank[g] = right
 
         def left_bias(g):
             lt = left_t_bank.pop(g)
@@ -264,6 +242,12 @@ def tile_mlstmblock_pa_t_kernel(
 
         def convolve_on_tensor(g):
             xlt = left_t.pop(g)
+            left = mpsum.tile([P, SUB, FEAT], F32, name="left")
+            for j in range(SUB):
+                nc.tensor.transpose(
+                    out=left[:, j, :], in_=xlt[:, j * P : (j + 1) * P], identity=ident[:]
+                )
+            left_bank[g] = left
             cvp = tpsum.tile([P, SUB_ON_TENSOR, FEAT], F32, name="cvp")
             for j in range(SUB_ON_TENSOR):
                 nc.tensor.matmul(
@@ -275,32 +259,40 @@ def tile_mlstmblock_pa_t_kernel(
                 )
             conv_bank[g] = cvp
 
-        def add_bias_and_convolve_last(g):
-            banks = row_banks.pop(g)
-            o = work.tile([P, 2, SUB, FEAT], F32, name="o")
+        def finish_rows(g):
+            left = left_bank.pop(g)
+            right = right_bank.pop(g)
+            o_left = work.tile([P, SUB, FEAT], F32, name="o_left")
+            nc.scalar.copy(out=o_left[:], in_=left[:])
+            nc.sync.dma_start(out=group_rows(out_0, g), in_=o_left[:])
             cv = work.tile([P, FEAT], F32, name="cv")
-            last_left = banks[SUB // 2 - 1][:, 1, 0:FEAT]
+            o_right = work.tile([P, SUB, FEAT], F32, name="o_right")
             for s in range(TAPS):
-                nc.vector.scalar_tensor_tensor(
-                    out=cv[:, s:FEAT],
-                    in0=last_left[:, 0 : FEAT - s],
-                    scalar=taps[:, TAPS - 1 - s : TAPS - s],
-                    in1=conv_of_bias[:] if s == 0 else cv[:, s:FEAT],
-                    op0=ALU.mult,
-                    op1=ALU.add,
-                )
-                if s < SUB // 2:
+                if s == 0:
+                    nc.vector.tensor_scalar(
+                        out=cv[:],
+                        in0=left[:, SUB - 1, :],
+                        scalar1=taps[:, TAPS - 1 : TAPS],
+                        scalar2=cbias[:, 0:1],
+                        op0=ALU.mult,
+                        op1=ALU.add,
+                    )
                     nc.vector.tensor_tensor(
-                        out=o[:, :, 2 * s : 2 * s + 2, :].rearrange("p l j n -> p j l n"),
-                        in0=banks[s][:].rearrange("p j (l n) -> p j l n", l=2),
-                        in1=bias_bc[:]
-                        .rearrange("p (l n) -> p l n", l=2)
-                        .unsqueeze(1)
-                        .to_broadcast([P, 2, 2, FEAT]),
+                        out=o_right[:],
+                        in0=right[:],
+                        in1=bias_bc[:].unsqueeze(1).to_broadcast([P, SUB, FEAT]),
                         op=ALU.add,
                     )
-            nc.sync.dma_start(out=group_rows(out_0, g), in_=o[:, 0, :, :])
-            nc.sync.dma_start(out=group_rows(out_2, g), in_=o[:, 1, :, :])
+                else:
+                    nc.vector.scalar_tensor_tensor(
+                        out=cv[:, s:FEAT],
+                        in0=left[:, SUB - 1, 0 : FEAT - s],
+                        scalar=taps[:, TAPS - 1 - s : TAPS - s],
+                        in1=cv[:, s:FEAT],
+                        op0=ALU.mult,
+                        op1=ALU.add,
+                    )
+            nc.sync.dma_start(out=group_rows(out_2, g), in_=o_right[:])
             conv_last[g] = cv
 
         def silu(g):
@@ -314,7 +306,7 @@ def tile_mlstmblock_pa_t_kernel(
             nc.sync.dma_start(out=group_rows(out_1, g), in_=xc[:])
 
         stats(0)
-        cols, w_codes, w_scales, bias_bc, taps, cbias, band, conv_of_bias = constants()
+        cols, w_codes, w_scales, bias_bc, taps, cbias, band = constants()
         for g in range(N_GROUPS):
             if g > 0:
                 stats(g)
@@ -326,5 +318,5 @@ def tile_mlstmblock_pa_t_kernel(
             project(g)
             left_bias(g)
             convolve_on_tensor(g)
-            add_bias_and_convolve_last(g)
+            finish_rows(g)
             silu(g)

@@ -19,7 +19,7 @@ SUB = 4
 GROUP_ROWS = P * SUB
 N_GROUPS = ROWS // GROUP_ROWS
 SUB_ON_TENSOR = 3
-ROWS_ON_SCALAR = 256
+ROWS_ON_SCALAR = 352
 
 FLOPS = 2 * ROWS * IN * 2 * FEAT
 
@@ -140,7 +140,7 @@ def tile_mlstmblock_pa_t_kernel(
             nc.gpsimd.tensor_tensor(out=rstd[:], in0=var_eps[:], in1=neg_half[:], op=ALU.pow)
             t = work.tile([P, SUB, IN], F32, name="t")
             for j in range(SUB):
-                nc.gpsimd.tensor_scalar(
+                nc.vector.tensor_scalar(
                     out=t[:, j, :].rearrange("p (c m) -> p c m", c=PACK),
                     in0=x_sb[g][:, j, :].rearrange("p (m c) -> p c m", c=PACK),
                     scalar1=neg_mean[:, j : j + 1],
@@ -180,13 +180,9 @@ def tile_mlstmblock_pa_t_kernel(
         def regroup(g):
             planes = planes_of.pop(g)
             grp = work.tile([P, GROUP_ROWS, PACK], BF16, name="grp", align_bytes=64)
-            nc.gpsimd.tensor_scalar(
-                out=grp[:, ROWS_ON_SCALAR:, :],
-                in0=planes[:, :, ROWS_ON_SCALAR:].rearrange("p c r -> p r c"),
-                scalar1=1.0,
-                scalar2=0.0,
-                op0=ALU.mult,
-                op1=ALU.add,
+            nc.vector.tensor_copy(
+                out=grp[:, ROWS_ON_SCALAR:, :].rearrange("p (q i) c -> p q c i", i=4),
+                in_=planes[:, :, ROWS_ON_SCALAR:].rearrange("p c (q i) -> p q c i", i=4),
             )
             nc.scalar.copy(
                 out=grp[:, 0:ROWS_ON_SCALAR, :].rearrange("p (q i) c -> p q c i", i=4),

@@ -19,7 +19,8 @@ SUB = 4
 GROUP_ROWS = P * SUB
 N_GROUPS = ROWS // GROUP_ROWS
 SUB_ON_TENSOR = 3
-ROWS_ON_SCALAR = 352
+SUB_ON_SCALAR = 3
+SCALAR_ROWS = P * SUB_ON_SCALAR
 
 FLOPS = 2 * ROWS * IN * 2 * FEAT
 
@@ -34,6 +35,7 @@ def tile_mlstmblock_pa_t_kernel(
         small = ctx.enter_context(tc.tile_pool(name="small", bufs=4))
         work = ctx.enter_context(tc.tile_pool(name="work", bufs=3))
         tpsum = ctx.enter_context(tc.psum_pool(name="tpsum", bufs=1))
+        bpsum = ctx.enter_context(tc.psum_pool(name="bpsum", bufs=3))
         mpsum = ctx.enter_context(tc.psum_pool(name="mpsum", bufs=1))
 
         def group_rows(dram, g):
@@ -132,7 +134,44 @@ def tile_mlstmblock_pa_t_kernel(
                     op0=ALU.mult,
                     op1=ALU.add,
                 )
-            return cols, w_codes, w_scales, bias_bc, taps, cbias, band
+            ln_w32, ln_b32 = cols[:, 0:PACK], cols[:, PACK : 2 * PACK]
+
+            def magnitude(v, name):
+                m = const.tile([P, PACK], F32, name=name)
+                nc.vector.tensor_scalar(out=m[:], in0=v, scalar1=-1.0, scalar2=None, op0=ALU.mult)
+                nc.vector.tensor_tensor(out=m[:], in0=m[:], in1=v, op=ALU.max)
+                return m
+
+            floor_w = magnitude(ln_b32, "floor_w")
+            nc.vector.tensor_scalar(
+                out=floor_w[:],
+                in0=floor_w[:],
+                scalar1=2.0**-60,
+                scalar2=2.0**-100,
+                op0=ALU.mult,
+                op1=ALU.max,
+            )
+            too_small = magnitude(ln_w32, "too_small")
+            nc.vector.tensor_tensor(
+                out=too_small[:], in0=too_small[:], in1=floor_w[:], op=ALU.is_lt
+            )
+            safe_w = const.tile([P, PACK], F32, name="safe_w")
+            nc.vector.tensor_tensor(out=safe_w[:], in0=floor_w[:], in1=ln_w32, op=ALU.subtract)
+            nc.vector.tensor_tensor(out=safe_w[:], in0=safe_w[:], in1=too_small[:], op=ALU.mult)
+            nc.vector.tensor_tensor(out=safe_w[:], in0=safe_w[:], in1=ln_w32, op=ALU.add)
+            shift = const.tile([P, PACK], F32, name="shift")
+            nc.vector.reciprocal(out=shift[:], in_=safe_w[:])
+            nc.vector.tensor_tensor(out=shift[:], in0=shift[:], in1=ln_b32, op=ALU.mult)
+            shift_ps = tpsum.tile([P, PACK, P], F32, name="shift_ps", tag="sums")
+            for c in range(PACK):
+                nc.tensor.transpose(
+                    out=shift_ps[:, c, :],
+                    in_=shift[:, c : c + 1].to_broadcast([P, P]),
+                    identity=ident[:],
+                )
+            shift_rows = const.tile([P, IN], F32, name="shift_rows")
+            nc.scalar.copy(out=shift_rows[:], in_=shift_ps[:].rearrange("p c m -> p (c m)"))
+            return cols, w_codes, w_scales, bias_bc, taps, cbias, band, safe_w, shift_rows
 
         def normalise(g):
             neg_mean, var_eps = mean_var.pop(g)
@@ -140,7 +179,7 @@ def tile_mlstmblock_pa_t_kernel(
             nc.gpsimd.tensor_tensor(out=rstd[:], in0=var_eps[:], in1=neg_half[:], op=ALU.pow)
             t = work.tile([P, SUB, IN], F32, name="t")
             for j in range(SUB):
-                nc.vector.tensor_scalar(
+                nc.gpsimd.tensor_scalar(
                     out=t[:, j, :].rearrange("p (c m) -> p c m", c=PACK),
                     in0=x_sb[g][:, j, :].rearrange("p (m c) -> p c m", c=PACK),
                     scalar1=neg_mean[:, j : j + 1],
@@ -152,21 +191,39 @@ def tile_mlstmblock_pa_t_kernel(
 
         def transpose(g):
             t = normed.pop(g)
-            banks = [
-                tpsum.tile([P, GROUP_ROWS], F32, name="bank", tag="tp%d" % c) for c in range(PACK)
-            ]
+            banks = []
             for c in range(PACK):
-                for j in range(SUB):
+                bank = bpsum.tile([P, SCALAR_ROWS], F32, name="bank")
+                for j in range(SUB_ON_SCALAR):
                     nc.tensor.transpose(
-                        out=banks[c][:, j * P : (j + 1) * P],
+                        out=bank[:, j * P : (j + 1) * P],
                         in_=t[:, j, c * P : (c + 1) * P],
                         identity=ident[:],
                     )
-            t_banks[g] = banks
+                banks.append(bank)
+            sums = tpsum.tile([P, PACK, P], F32, name="sums", tag="sums")
+            for c in range(PACK):
+                for addend, first in ((t[:, SUB_ON_SCALAR, :], True), (shift_rows[:], False)):
+                    nc.tensor.matmul(
+                        out=sums[:, c, :],
+                        lhsT=addend[:, c * P : (c + 1) * P],
+                        rhs=ident[:],
+                        start=first,
+                        stop=not first,
+                        is_transpose=True,
+                    )
+            t_banks[g] = banks, sums
 
         def scale_shift(g):
-            banks = t_banks.pop(g)
-            planes = work.tile([P, PACK, GROUP_ROWS], BF16, name="planes")
+            banks, sums = t_banks.pop(g)
+            grp = work.tile([P, GROUP_ROWS, PACK], BF16, name="grp", align_bytes=64)
+            nc.vector.tensor_tensor(
+                out=grp[:, SCALAR_ROWS:, :],
+                in0=sums[:].rearrange("p c r -> p r c"),
+                in1=safe_w[:].unsqueeze(1).to_broadcast([P, P, PACK]),
+                op=ALU.mult,
+            )
+            planes = work.tile([P, PACK, SCALAR_ROWS], BF16, name="planes")
             for c in range(PACK):
                 nc.scalar.activation(
                     out=planes[:, c, :],
@@ -175,18 +232,13 @@ def tile_mlstmblock_pa_t_kernel(
                     scale=cols[:, c : c + 1],
                     bias=cols[:, PACK + c : PACK + c + 1],
                 )
-            planes_of[g] = planes
+            planes_of[g] = planes, grp
 
         def regroup(g):
-            planes = planes_of.pop(g)
-            grp = work.tile([P, GROUP_ROWS, PACK], BF16, name="grp", align_bytes=64)
-            nc.vector.tensor_copy(
-                out=grp[:, ROWS_ON_SCALAR:, :].rearrange("p (q i) c -> p q c i", i=4),
-                in_=planes[:, :, ROWS_ON_SCALAR:].rearrange("p c (q i) -> p q c i", i=4),
-            )
+            planes, grp = planes_of.pop(g)
             nc.scalar.copy(
-                out=grp[:, 0:ROWS_ON_SCALAR, :].rearrange("p (q i) c -> p q c i", i=4),
-                in_=planes[:, :, 0:ROWS_ON_SCALAR].rearrange("p c (q i) -> p q c i", i=4),
+                out=grp[:, 0:SCALAR_ROWS, :].rearrange("p (q i) c -> p q c i", i=4),
+                in_=planes[:].rearrange("p c (q i) -> p q c i", i=4),
             )
             grouped[g] = grp
 
@@ -238,7 +290,7 @@ def tile_mlstmblock_pa_t_kernel(
 
         def convolve_on_tensor(g):
             xlt = left_t.pop(g)
-            left = mpsum.tile([P, SUB, FEAT], F32, name="left")
+            left = tpsum.tile([P, SUB, FEAT], F32, name="left")
             for j in range(SUB):
                 nc.tensor.transpose(
                     out=left[:, j, :], in_=xlt[:, j * P : (j + 1) * P], identity=ident[:]
@@ -302,7 +354,7 @@ def tile_mlstmblock_pa_t_kernel(
             nc.sync.dma_start(out=group_rows(out_1, g), in_=xc[:])
 
         stats(0)
-        cols, w_codes, w_scales, bias_bc, taps, cbias, band = constants()
+        cols, w_codes, w_scales, bias_bc, taps, cbias, band, safe_w, shift_rows = constants()
         for g in range(N_GROUPS):
             if g > 0:
                 stats(g)

@@ -18,11 +18,14 @@ EPS = 1e-5
 SUB = 4
 GROUP_ROWS = P * SUB
 N_GROUPS = ROWS // GROUP_ROWS
-SUB_ON_TENSOR = 3
 SUB_ON_SCALAR = 3
 SCALAR_ROWS = P * SUB_ON_SCALAR
 
 FLOPS = 2 * ROWS * IN * 2 * FEAT
+
+
+def row_tiles_convolved_on_tensor(g):
+    return SUB // 2 if g % 2 == 1 and g < N_GROUPS - 1 else SUB
 
 
 def tile_mlstmblock_pa_t_kernel(
@@ -31,27 +34,26 @@ def tile_mlstmblock_pa_t_kernel(
     nc = tc.nc
     with ExitStack() as ctx:
         const = ctx.enter_context(tc.tile_pool(name="const", bufs=1))
-        xin = ctx.enter_context(tc.tile_pool(name="xin", bufs=1))
         small = ctx.enter_context(tc.tile_pool(name="small", bufs=4))
         work = ctx.enter_context(tc.tile_pool(name="work", bufs=3))
-        tpsum = ctx.enter_context(tc.psum_pool(name="tpsum", bufs=1))
-        bpsum = ctx.enter_context(tc.psum_pool(name="bpsum", bufs=3))
-        mpsum = ctx.enter_context(tc.psum_pool(name="mpsum", bufs=1))
+        slots = ctx.enter_context(tc.psum_pool(name="slots", bufs=3))
+        psum = ctx.enter_context(tc.psum_pool(name="psum", bufs=1))
 
         def group_rows(dram, g):
             return dram[g * GROUP_ROWS : (g + 1) * GROUP_ROWS, :].rearrange(
                 "(p j) n -> p j n", j=SUB
             )
 
-        x_sb = [xin.tile([P, SUB, IN], BF16, name="x%d" % g) for g in range(N_GROUPS)]
-        for g in range(N_GROUPS):
+        x_sb = [const.tile([P, SUB, IN], BF16, name="x%d" % g) for g in range(N_GROUPS)]
+
+        def load(g):
             nc.sync.dma_start(out=x_sb[g][:], in_=group_rows(x, g))
+
+        load(0)
         lnw_bf = const.tile([P, PACK], BF16, name="lnw_bf")
         nc.scalar.dma_start(out=lnw_bf[:], in_=ln_w.rearrange("(p c) -> p c", c=PACK))
         lnb_bf = const.tile([P, PACK], BF16, name="lnb_bf")
         nc.scalar.dma_start(out=lnb_bf[:], in_=ln_b.rearrange("(p c) -> p c", c=PACK))
-        lbias_bf = const.tile([P, 1], BF16, name="lbias_bf")
-        nc.scalar.dma_start(out=lbias_bf[:], in_=upL_b.rearrange("(p c) -> p c", c=1))
         w_raw = const.tile([P, PACK, 2 * FEAT], BF16, name="w_raw")
         nc.scalar.dma_start(
             out=w_raw[:, :, 0:FEAT], in_=upL_w.rearrange("(p c) n -> p c n", c=PACK)
@@ -59,17 +61,30 @@ def tile_mlstmblock_pa_t_kernel(
         nc.scalar.dma_start(
             out=w_raw[:, :, FEAT : 2 * FEAT], in_=upR_w.rearrange("(p c) n -> p c n", c=PACK)
         )
+        lbias_bf = const.tile([P, 1], BF16, name="lbias_bf")
+        nc.scalar.dma_start(out=lbias_bf[:], in_=upL_b.rearrange("(p c) -> p c", c=1))
         bias_bf = const.tile([P, FEAT], BF16, name="bias_bf")
         nc.scalar.dma_start(out=bias_bf[:], in_=upR_b.partition_broadcast(P))
         taps_bf = const.tile([P, TAPS], BF16, name="taps_bf")
         nc.scalar.dma_start(out=taps_bf[:], in_=conv_w.partition_broadcast(P))
         cbias_bf = const.tile([P, 1], BF16, name="cbias_bf")
         nc.scalar.dma_start(out=cbias_bf[:], in_=conv_b.partition_broadcast(P))
+        for g in range(1, N_GROUPS):
+            load(g)
 
-        ident = const.tile([P, P], F32, name="ident")
-        make_identity(nc, ident[:])
         neg_half = const.tile([P, SUB], F32, name="neg_half")
         nc.gpsimd.memset(neg_half[:], -0.5)
+        ident = const.tile([P, P], F32, name="ident")
+        make_identity(nc, ident[:])
+        first_silu = const.tile([P, 1], F32, name="first_silu")
+        nc.scalar.activation(out=first_silu[:], in_=neg_half[:, 0:1], func=ACT.Silu)
+
+        row_stats = []
+        for k in range(2):
+            st = const.tile([P, SUB, 9], F32, name="st%d" % k)
+            nc.vector.memset(st[:], 0.0)
+            nc.vector.memset(st[:, :, 8], IN * EPS)
+            row_stats.append(st)
 
         mean_var = {}
         normed = {}
@@ -77,63 +92,49 @@ def tile_mlstmblock_pa_t_kernel(
         planes_of = {}
         grouped = {}
         mx_words = {}
-        right_bank = {}
-        left_bank = {}
         left_t_bank = {}
+        right_bank = {}
         left_t = {}
+        left_bank = {}
         conv_bank = {}
-        conv_last = {}
+        conv_rest = {}
 
         def stats(g):
-            st = small.tile([P, SUB, 6], F32, name="st")
+            st = row_stats[g % 2]
             mv = small.tile([P, SUB, 2], F32, name="mv")
             for j in range(SUB):
-                nc.vector.bn_stats(out=st[:, j, :], in_=x_sb[g][:, j, :])
-            for j in range(SUB):
-                nc.vector.bn_aggr(out=mv[:, j, :], in_=st[:, j, :])
-            var_eps = small.tile([P, SUB], F32, name="var_eps")
-            nc.vector.tensor_scalar(
-                out=var_eps[:], in0=mv[:, :, 1], scalar1=EPS, scalar2=None, op0=ALU.add
-            )
+                nc.vector.bn_stats(out=st[:, j, 0:6], in_=x_sb[g][:, j, :])
             neg_mean = small.tile([P, SUB], F32, name="neg_mean")
-            nc.vector.tensor_scalar(
-                out=neg_mean[:], in0=mv[:, :, 0], scalar1=-1.0, scalar2=None, op0=ALU.mult
-            )
-            mean_var[g] = (neg_mean, var_eps)
+            with tc.high_priority(offset=1000):
+                for j in range(SUB):
+                    nc.vector.bn_aggr(out=mv[:, j, :], in_=st[:, j, :])
+                nc.vector.tensor_scalar(
+                    out=neg_mean[:], in0=mv[:, :, 0], scalar1=-1.0, scalar2=None, op0=ALU.mult
+                )
+            mean_var[g] = (neg_mean, mv)
 
-        def constants():
+        def normalise(g):
+            neg_mean, mv = mean_var.pop(g)
+            rstd = small.tile([P, SUB], F32, name="rstd")
+            nc.gpsimd.tensor_tensor(out=rstd[:], in0=mv[:, :, 1], in1=neg_half[:], op=ALU.pow)
+            t = work.tile([P, SUB, IN], F32, name="t")
+            for j in range(SUB):
+                engine = nc.vector if j >= SUB_ON_SCALAR else nc.gpsimd
+                engine.tensor_scalar(
+                    out=t[:, j, :].rearrange("p (c m) -> p c m", c=PACK),
+                    in0=x_sb[g][:, j, :].rearrange("p (m c) -> p c m", c=PACK),
+                    scalar1=neg_mean[:, j : j + 1],
+                    scalar2=rstd[:, j : j + 1],
+                    op0=ALU.add,
+                    op1=ALU.mult,
+                )
+            normed[g] = t
+
+        def norm_constants():
             cols = const.tile([P, 2 * PACK + 1], F32, name="cols")
             nc.vector.tensor_copy(out=cols[:, 0:PACK], in_=lnw_bf[:])
             nc.vector.tensor_copy(out=cols[:, PACK : 2 * PACK], in_=lnb_bf[:])
             nc.vector.tensor_copy(out=cols[:, 2 * PACK : 2 * PACK + 1], in_=lbias_bf[:])
-            w_grouped = const.tile([P, 2 * FEAT, PACK], BF16, name="w_grouped", align_bytes=64)
-            nc.vector.tensor_copy(out=w_grouped[:], in_=w_raw[:].rearrange("p c n -> p n c"))
-            w_codes = const.tile([P, 2 * FEAT], U32, name="w_codes", align_bytes=64)
-            w_scales = const.tile([P, 2 * FEAT], U8, name="w_scales", align_bytes=64)
-            bias_bc = const.tile([P, FEAT], F32, name="bias_bc")
-            nc.vector.tensor_copy(out=bias_bc[:], in_=bias_bf[:])
-            nc.vector.quantize_mx(
-                out=w_codes[:].bitcast(FP8X4),
-                scales=w_scales[:],
-                in_=w_grouped[:].rearrange("p n c -> p (n c)"),
-            )
-            taps = const.tile([P, TAPS], F32, name="taps")
-            nc.vector.tensor_copy(out=taps[:], in_=taps_bf[:])
-            cbias = const.tile([P, 1], F32, name="cbias")
-            nc.vector.tensor_copy(out=cbias[:], in_=cbias_bf[:])
-            band = const.tile([P, FEAT], F32, name="band")
-            nc.vector.tensor_scalar(
-                out=band[:], in0=ident[:], scalar1=taps[:, TAPS - 1 : TAPS], scalar2=None, op0=ALU.mult
-            )
-            for s in range(1, TAPS):
-                nc.vector.scalar_tensor_tensor(
-                    out=band[:, s:FEAT],
-                    in0=ident[:, 0 : FEAT - s],
-                    scalar=taps[:, TAPS - 1 - s : TAPS - s],
-                    in1=band[:, s:FEAT],
-                    op0=ALU.mult,
-                    op1=ALU.add,
-                )
             ln_w32, ln_b32 = cols[:, 0:PACK], cols[:, PACK : 2 * PACK]
 
             def magnitude(v, name):
@@ -162,7 +163,7 @@ def tile_mlstmblock_pa_t_kernel(
             shift = const.tile([P, PACK], F32, name="shift")
             nc.vector.reciprocal(out=shift[:], in_=safe_w[:])
             nc.vector.tensor_tensor(out=shift[:], in0=shift[:], in1=ln_b32, op=ALU.mult)
-            shift_ps = tpsum.tile([P, PACK, P], F32, name="shift_ps", tag="sums")
+            shift_ps = psum.tile([P, PACK, P], F32, name="shift_ps", tag="sums")
             for c in range(PACK):
                 nc.tensor.transpose(
                     out=shift_ps[:, c, :],
@@ -171,29 +172,44 @@ def tile_mlstmblock_pa_t_kernel(
                 )
             shift_rows = const.tile([P, IN], F32, name="shift_rows")
             nc.scalar.copy(out=shift_rows[:], in_=shift_ps[:].rearrange("p c m -> p (c m)"))
-            return cols, w_codes, w_scales, bias_bc, taps, cbias, band, safe_w, shift_rows
+            return cols, safe_w, shift_rows
 
-        def normalise(g):
-            neg_mean, var_eps = mean_var.pop(g)
-            rstd = small.tile([P, SUB], F32, name="rstd")
-            nc.gpsimd.tensor_tensor(out=rstd[:], in0=var_eps[:], in1=neg_half[:], op=ALU.pow)
-            t = work.tile([P, SUB, IN], F32, name="t")
-            for j in range(SUB):
-                nc.gpsimd.tensor_scalar(
-                    out=t[:, j, :].rearrange("p (c m) -> p c m", c=PACK),
-                    in0=x_sb[g][:, j, :].rearrange("p (m c) -> p c m", c=PACK),
-                    scalar1=neg_mean[:, j : j + 1],
-                    scalar2=rstd[:, j : j + 1],
-                    op0=ALU.add,
-                    op1=ALU.mult,
+        def product_constants():
+            w_grouped = const.tile([P, 2 * FEAT, PACK], BF16, name="w_grouped", align_bytes=64)
+            nc.vector.tensor_copy(out=w_grouped[:], in_=w_raw[:].rearrange("p c n -> p n c"))
+            taps = const.tile([P, TAPS], F32, name="taps")
+            nc.vector.tensor_copy(out=taps[:], in_=taps_bf[:])
+            cbias = const.tile([P, 1], F32, name="cbias")
+            nc.vector.tensor_copy(out=cbias[:], in_=cbias_bf[:])
+            bias_bc = const.tile([P, FEAT], F32, name="bias_bc")
+            nc.vector.tensor_copy(out=bias_bc[:], in_=bias_bf[:])
+            w_codes = const.tile([P, 2 * FEAT], U32, name="w_codes", align_bytes=64)
+            w_scales = const.tile([P, 2 * FEAT], U8, name="w_scales", align_bytes=64)
+            nc.vector.quantize_mx(
+                out=w_codes[:].bitcast(FP8X4),
+                scales=w_scales[:],
+                in_=w_grouped[:].rearrange("p n c -> p (n c)"),
+            )
+            band = const.tile([P, FEAT], F32, name="band")
+            nc.vector.tensor_scalar(
+                out=band[:], in0=ident[:], scalar1=taps[:, TAPS - 1 : TAPS], scalar2=None, op0=ALU.mult
+            )
+            for s in range(1, TAPS):
+                nc.vector.scalar_tensor_tensor(
+                    out=band[:, s:FEAT],
+                    in0=ident[:, 0 : FEAT - s],
+                    scalar=taps[:, TAPS - 1 - s : TAPS - s],
+                    in1=band[:, s:FEAT],
+                    op0=ALU.mult,
+                    op1=ALU.add,
                 )
-            normed[g] = t
+            return w_codes, w_scales, bias_bc, taps, cbias, band
 
         def transpose(g):
             t = normed.pop(g)
             banks = []
             for c in range(PACK):
-                bank = bpsum.tile([P, SCALAR_ROWS], F32, name="bank")
+                bank = slots.tile([P, SCALAR_ROWS], F32, name="bank")
                 for j in range(SUB_ON_SCALAR):
                     nc.tensor.transpose(
                         out=bank[:, j * P : (j + 1) * P],
@@ -201,7 +217,7 @@ def tile_mlstmblock_pa_t_kernel(
                         identity=ident[:],
                     )
                 banks.append(bank)
-            sums = tpsum.tile([P, PACK, P], F32, name="sums", tag="sums")
+            sums = psum.tile([P, PACK, P], F32, name="sums", tag="sums")
             for c in range(PACK):
                 for addend, first in ((t[:, SUB_ON_SCALAR, :], True), (shift_rows[:], False)):
                     nc.tensor.matmul(
@@ -215,14 +231,7 @@ def tile_mlstmblock_pa_t_kernel(
             t_banks[g] = banks, sums
 
         def scale_shift(g):
-            banks, sums = t_banks.pop(g)
-            grp = work.tile([P, GROUP_ROWS, PACK], BF16, name="grp", align_bytes=64)
-            nc.vector.tensor_tensor(
-                out=grp[:, SCALAR_ROWS:, :],
-                in0=sums[:].rearrange("p c r -> p r c"),
-                in1=safe_w[:].unsqueeze(1).to_broadcast([P, P, PACK]),
-                op=ALU.mult,
-            )
+            banks, sums = t_banks[g]
             planes = work.tile([P, PACK, SCALAR_ROWS], BF16, name="planes")
             for c in range(PACK):
                 nc.scalar.activation(
@@ -232,15 +241,25 @@ def tile_mlstmblock_pa_t_kernel(
                     scale=cols[:, c : c + 1],
                     bias=cols[:, PACK + c : PACK + c + 1],
                 )
-            planes_of[g] = planes, grp
+            planes_of[g] = planes
 
         def regroup(g):
-            planes, grp = planes_of.pop(g)
+            planes = planes_of.pop(g)
+            grp = work.tile([P, GROUP_ROWS, PACK], BF16, name="grp", align_bytes=64)
             nc.scalar.copy(
                 out=grp[:, 0:SCALAR_ROWS, :].rearrange("p (q i) c -> p q c i", i=4),
                 in_=planes[:].rearrange("p c (q i) -> p q c i", i=4),
             )
             grouped[g] = grp
+
+        def scale_sums(g):
+            banks, sums = t_banks.pop(g)
+            nc.vector.tensor_tensor(
+                out=grouped[g][:, SCALAR_ROWS:, :],
+                in0=sums[:].rearrange("p c r -> p r c"),
+                in1=safe_w[:].unsqueeze(1).to_broadcast([P, P, PACK]),
+                op=ALU.mult,
+            )
 
         def quantise(g):
             grp = grouped.pop(g)
@@ -255,7 +274,7 @@ def tile_mlstmblock_pa_t_kernel(
 
         def project(g):
             codes, scales = mx_words.pop(g)
-            lt = tpsum.tile([P, GROUP_ROWS], F32, name="lt")
+            lt = psum.tile([P, GROUP_ROWS], F32, name="lt")
             nc.tensor.matmul_mx(
                 out=lt[:],
                 lhsT=w_codes[:, 0:FEAT].bitcast(FP8X4),
@@ -266,7 +285,7 @@ def tile_mlstmblock_pa_t_kernel(
                 stop=True,
             )
             left_t_bank[g] = lt
-            right = mpsum.tile([P, SUB, FEAT], F32, name="right")
+            right = psum.tile([P, SUB, FEAT], F32, name="right")
             for j in range(SUB):
                 sub_cols = slice(j * P, (j + 1) * P)
                 nc.tensor.matmul_mx(
@@ -288,16 +307,18 @@ def tile_mlstmblock_pa_t_kernel(
             )
             left_t[g] = xlt
 
-        def convolve_on_tensor(g):
-            xlt = left_t.pop(g)
-            left = tpsum.tile([P, SUB, FEAT], F32, name="left")
+        def left_rows(g):
+            left = psum.tile([P, SUB, FEAT], F32, name="left")
             for j in range(SUB):
                 nc.tensor.transpose(
-                    out=left[:, j, :], in_=xlt[:, j * P : (j + 1) * P], identity=ident[:]
+                    out=left[:, j, :], in_=left_t[g][:, j * P : (j + 1) * P], identity=ident[:]
                 )
             left_bank[g] = left
-            cvp = tpsum.tile([P, SUB_ON_TENSOR, FEAT], F32, name="cvp")
-            for j in range(SUB_ON_TENSOR):
+
+        def convolve_on_tensor(g):
+            xlt = left_t.pop(g)
+            cvp = psum.tile([P, SUB, FEAT], F32, name="cvp")
+            for j in range(row_tiles_convolved_on_tensor(g)):
                 nc.tensor.matmul(
                     out=cvp[:, j, :],
                     lhsT=xlt[:, j * P : (j + 1) * P],
@@ -307,54 +328,62 @@ def tile_mlstmblock_pa_t_kernel(
                 )
             conv_bank[g] = cvp
 
-        def finish_rows(g):
-            left = left_bank.pop(g)
-            right = right_bank.pop(g)
+        def convolve_on_vector(g):
+            left = left_bank[g]
+            first = row_tiles_convolved_on_tensor(g)
+            if first == SUB:
+                return
+            cv = work.tile([P, SUB - first, FEAT], F32, name="cv")
+            nc.vector.tensor_scalar(
+                out=cv[:],
+                in0=left[:, first:, :],
+                scalar1=taps[:, TAPS - 1 : TAPS],
+                scalar2=cbias[:, 0:1],
+                op0=ALU.mult,
+                op1=ALU.add,
+            )
+            for s in range(1, TAPS):
+                nc.vector.scalar_tensor_tensor(
+                    out=cv[:, :, s:FEAT],
+                    in0=left[:, first:, 0 : FEAT - s],
+                    scalar=taps[:, TAPS - 1 - s : TAPS - s],
+                    in1=cv[:, :, s:FEAT],
+                    op0=ALU.mult,
+                    op1=ALU.add,
+                )
+            conv_rest[g] = cv
+
+        def left_out(g):
+            left = left_bank[g]
             o_left = work.tile([P, SUB, FEAT], F32, name="o_left")
             nc.scalar.copy(out=o_left[:], in_=left[:])
             nc.sync.dma_start(out=group_rows(out_0, g), in_=o_left[:])
-            cv = work.tile([P, FEAT], F32, name="cv")
+
+        def right_out(g):
+            right = right_bank.pop(g)
             o_right = work.tile([P, SUB, FEAT], F32, name="o_right")
-            for s in range(TAPS):
-                if s == 0:
-                    nc.vector.tensor_scalar(
-                        out=cv[:],
-                        in0=left[:, SUB - 1, :],
-                        scalar1=taps[:, TAPS - 1 : TAPS],
-                        scalar2=cbias[:, 0:1],
-                        op0=ALU.mult,
-                        op1=ALU.add,
-                    )
-                    nc.vector.tensor_tensor(
-                        out=o_right[:],
-                        in0=right[:],
-                        in1=bias_bc[:].unsqueeze(1).to_broadcast([P, SUB, FEAT]),
-                        op=ALU.add,
-                    )
-                else:
-                    nc.vector.scalar_tensor_tensor(
-                        out=cv[:, s:FEAT],
-                        in0=left[:, SUB - 1, 0 : FEAT - s],
-                        scalar=taps[:, TAPS - 1 - s : TAPS - s],
-                        in1=cv[:, s:FEAT],
-                        op0=ALU.mult,
-                        op1=ALU.add,
-                    )
+            nc.vector.tensor_tensor(
+                out=o_right[:],
+                in0=right[:],
+                in1=bias_bc[:].unsqueeze(1).to_broadcast([P, SUB, FEAT]),
+                op=ALU.add,
+            )
             nc.sync.dma_start(out=group_rows(out_2, g), in_=o_right[:])
-            conv_last[g] = cv
 
         def silu(g):
             cvp = conv_bank.pop(g)
-            cv = conv_last.pop(g)
+            first = row_tiles_convolved_on_tensor(g)
             xc = work.tile([P, SUB, FEAT], F32, name="xc")
             nc.scalar.activation(
-                out=xc[:, 0:SUB_ON_TENSOR, :], in_=cvp[:], func=ACT.Silu, bias=cbias[:, 0:1]
+                out=xc[:, 0:first, :], in_=cvp[:, 0:first, :], func=ACT.Silu, bias=cbias[:, 0:1]
             )
-            nc.scalar.activation(out=xc[:, SUB_ON_TENSOR, :], in_=cv[:], func=ACT.Silu)
+            if first < SUB:
+                nc.scalar.activation(out=xc[:, first:, :], in_=conv_rest.pop(g)[:], func=ACT.Silu)
             nc.sync.dma_start(out=group_rows(out_1, g), in_=xc[:])
 
         stats(0)
-        cols, w_codes, w_scales, bias_bc, taps, cbias, band, safe_w, shift_rows = constants()
+        cols, safe_w, shift_rows = norm_constants()
+        w_codes, w_scales, bias_bc, taps, cbias, band = product_constants()
         for g in range(N_GROUPS):
             if g > 0:
                 stats(g)
@@ -362,9 +391,13 @@ def tile_mlstmblock_pa_t_kernel(
             transpose(g)
             scale_shift(g)
             regroup(g)
+            scale_sums(g)
             quantise(g)
             project(g)
             left_bias(g)
+            left_rows(g)
             convolve_on_tensor(g)
-            finish_rows(g)
+            left_out(g)
+            right_out(g)
+            convolve_on_vector(g)
             silu(g)

@@ -18,10 +18,12 @@ EPS = 1e-5
 SUB = 4
 GROUP_ROWS = P * SUB
 N_GROUPS = ROWS // GROUP_ROWS
-SUB_ON_SCALAR = 3
-SCALAR_ROWS = P * SUB_ON_SCALAR
 
 FLOPS = 2 * ROWS * IN * 2 * FEAT
+
+
+def normaliser(nc, g, j):
+    return (nc.vector, nc.vector, nc.scalar, (nc.scalar, nc.gpsimd)[g % 2])[j]
 
 
 def row_tiles_convolved_on_tensor(g):
@@ -36,7 +38,7 @@ def tile_mlstmblock_pa_t_kernel(
         const = ctx.enter_context(tc.tile_pool(name="const", bufs=1))
         small = ctx.enter_context(tc.tile_pool(name="small", bufs=4))
         work = ctx.enter_context(tc.tile_pool(name="work", bufs=3))
-        slots = ctx.enter_context(tc.psum_pool(name="slots", bufs=3))
+        slots = ctx.enter_context(tc.psum_pool(name="slots", bufs=4))
         psum = ctx.enter_context(tc.psum_pool(name="psum", bufs=1))
 
         def group_rows(dram, g):
@@ -117,17 +119,30 @@ def tile_mlstmblock_pa_t_kernel(
             neg_mean, mv = mean_var.pop(g)
             rstd = small.tile([P, SUB], F32, name="rstd")
             nc.gpsimd.tensor_tensor(out=rstd[:], in0=mv[:, :, 1], in1=neg_half[:], op=ALU.pow)
+            shift = small.tile([P, SUB], F32, name="shift")
+            nc.gpsimd.tensor_tensor(out=shift[:], in0=neg_mean[:], in1=rstd[:], op=ALU.mult)
             t = work.tile([P, SUB, IN], F32, name="t")
             for j in range(SUB):
-                engine = nc.vector if j >= SUB_ON_SCALAR else nc.gpsimd
-                engine.tensor_scalar(
-                    out=t[:, j, :].rearrange("p (c m) -> p c m", c=PACK),
-                    in0=x_sb[g][:, j, :].rearrange("p (m c) -> p c m", c=PACK),
-                    scalar1=neg_mean[:, j : j + 1],
-                    scalar2=rstd[:, j : j + 1],
-                    op0=ALU.add,
-                    op1=ALU.mult,
-                )
+                t_j = t[:, j, :].rearrange("p (c m) -> p c m", c=PACK)
+                x_j = x_sb[g][:, j, :].rearrange("p (m c) -> p c m", c=PACK)
+                engine = normaliser(nc, g, j)
+                if engine != nc.scalar:
+                    engine.tensor_scalar(
+                        out=t_j,
+                        in0=x_j,
+                        scalar1=neg_mean[:, j : j + 1],
+                        scalar2=rstd[:, j : j + 1],
+                        op0=ALU.add,
+                        op1=ALU.mult,
+                    )
+                else:
+                    nc.scalar.activation(
+                        out=t_j,
+                        in_=x_j,
+                        func=ACT.Identity,
+                        scale=rstd[:, j : j + 1],
+                        bias=shift[:, j : j + 1],
+                    )
             normed[g] = t
 
         def norm_constants():
@@ -135,44 +150,7 @@ def tile_mlstmblock_pa_t_kernel(
             nc.vector.tensor_copy(out=cols[:, 0:PACK], in_=lnw_bf[:])
             nc.vector.tensor_copy(out=cols[:, PACK : 2 * PACK], in_=lnb_bf[:])
             nc.vector.tensor_copy(out=cols[:, 2 * PACK : 2 * PACK + 1], in_=lbias_bf[:])
-            ln_w32, ln_b32 = cols[:, 0:PACK], cols[:, PACK : 2 * PACK]
-
-            def magnitude(v, name):
-                m = const.tile([P, PACK], F32, name=name)
-                nc.vector.tensor_scalar(out=m[:], in0=v, scalar1=-1.0, scalar2=None, op0=ALU.mult)
-                nc.vector.tensor_tensor(out=m[:], in0=m[:], in1=v, op=ALU.max)
-                return m
-
-            floor_w = magnitude(ln_b32, "floor_w")
-            nc.vector.tensor_scalar(
-                out=floor_w[:],
-                in0=floor_w[:],
-                scalar1=2.0**-60,
-                scalar2=2.0**-100,
-                op0=ALU.mult,
-                op1=ALU.max,
-            )
-            too_small = magnitude(ln_w32, "too_small")
-            nc.vector.tensor_tensor(
-                out=too_small[:], in0=too_small[:], in1=floor_w[:], op=ALU.is_lt
-            )
-            safe_w = const.tile([P, PACK], F32, name="safe_w")
-            nc.vector.tensor_tensor(out=safe_w[:], in0=floor_w[:], in1=ln_w32, op=ALU.subtract)
-            nc.vector.tensor_tensor(out=safe_w[:], in0=safe_w[:], in1=too_small[:], op=ALU.mult)
-            nc.vector.tensor_tensor(out=safe_w[:], in0=safe_w[:], in1=ln_w32, op=ALU.add)
-            shift = const.tile([P, PACK], F32, name="shift")
-            nc.vector.reciprocal(out=shift[:], in_=safe_w[:])
-            nc.vector.tensor_tensor(out=shift[:], in0=shift[:], in1=ln_b32, op=ALU.mult)
-            shift_ps = psum.tile([P, PACK, P], F32, name="shift_ps", tag="sums")
-            for c in range(PACK):
-                nc.tensor.transpose(
-                    out=shift_ps[:, c, :],
-                    in_=shift[:, c : c + 1].to_broadcast([P, P]),
-                    identity=ident[:],
-                )
-            shift_rows = const.tile([P, IN], F32, name="shift_rows")
-            nc.scalar.copy(out=shift_rows[:], in_=shift_ps[:].rearrange("p c m -> p (c m)"))
-            return cols, safe_w, shift_rows
+            return cols
 
         def product_constants():
             w_grouped = const.tile([P, 2 * FEAT, PACK], BF16, name="w_grouped", align_bytes=64)
@@ -209,30 +187,19 @@ def tile_mlstmblock_pa_t_kernel(
             t = normed.pop(g)
             banks = []
             for c in range(PACK):
-                bank = slots.tile([P, SCALAR_ROWS], F32, name="bank")
-                for j in range(SUB_ON_SCALAR):
+                bank = slots.tile([P, GROUP_ROWS], F32, name="bank")
+                for j in range(SUB):
                     nc.tensor.transpose(
                         out=bank[:, j * P : (j + 1) * P],
                         in_=t[:, j, c * P : (c + 1) * P],
                         identity=ident[:],
                     )
                 banks.append(bank)
-            sums = psum.tile([P, PACK, P], F32, name="sums", tag="sums")
-            for c in range(PACK):
-                for addend, first in ((t[:, SUB_ON_SCALAR, :], True), (shift_rows[:], False)):
-                    nc.tensor.matmul(
-                        out=sums[:, c, :],
-                        lhsT=addend[:, c * P : (c + 1) * P],
-                        rhs=ident[:],
-                        start=first,
-                        stop=not first,
-                        is_transpose=True,
-                    )
-            t_banks[g] = banks, sums
+            t_banks[g] = banks
 
         def scale_shift(g):
-            banks, sums = t_banks[g]
-            planes = work.tile([P, PACK, SCALAR_ROWS], BF16, name="planes")
+            banks = t_banks.pop(g)
+            planes = work.tile([P, PACK, GROUP_ROWS], BF16, name="planes")
             for c in range(PACK):
                 nc.scalar.activation(
                     out=planes[:, c, :],
@@ -246,20 +213,15 @@ def tile_mlstmblock_pa_t_kernel(
         def regroup(g):
             planes = planes_of.pop(g)
             grp = work.tile([P, GROUP_ROWS, PACK], BF16, name="grp", align_bytes=64)
-            nc.scalar.copy(
-                out=grp[:, 0:SCALAR_ROWS, :].rearrange("p (q i) c -> p q c i", i=4),
-                in_=planes[:].rearrange("p c (q i) -> p q c i", i=4),
+            nc.gpsimd.tensor_scalar(
+                out=grp[:],
+                in0=planes[:].rearrange("p c r -> p r c"),
+                scalar1=1.0,
+                scalar2=0.0,
+                op0=ALU.mult,
+                op1=ALU.add,
             )
             grouped[g] = grp
-
-        def scale_sums(g):
-            banks, sums = t_banks.pop(g)
-            nc.vector.tensor_tensor(
-                out=grouped[g][:, SCALAR_ROWS:, :],
-                in0=sums[:].rearrange("p c r -> p r c"),
-                in1=safe_w[:].unsqueeze(1).to_broadcast([P, P, PACK]),
-                op=ALU.mult,
-            )
 
         def quantise(g):
             grp = grouped.pop(g)
@@ -382,16 +344,17 @@ def tile_mlstmblock_pa_t_kernel(
             nc.sync.dma_start(out=group_rows(out_1, g), in_=xc[:])
 
         stats(0)
-        cols, safe_w, shift_rows = norm_constants()
+        cols = norm_constants()
         w_codes, w_scales, bias_bc, taps, cbias, band = product_constants()
+        with tc.high_priority(offset=1000):
+            normalise(0)
         for g in range(N_GROUPS):
-            if g > 0:
-                stats(g)
-            normalise(g)
+            if g + 1 < N_GROUPS:
+                stats(g + 1)
+                normalise(g + 1)
             transpose(g)
             scale_shift(g)
             regroup(g)
-            scale_sums(g)
             quantise(g)
             project(g)
             left_bias(g)

@@ -56,21 +56,21 @@ def tile_mlstmblock_pa_t_kernel(
         nc.scalar.dma_start(out=lnw_bf[:], in_=ln_w.rearrange("(p c) -> p c", c=PACK))
         lnb_bf = const.tile([P, PACK], BF16, name="lnb_bf")
         nc.scalar.dma_start(out=lnb_bf[:], in_=ln_b.rearrange("(p c) -> p c", c=PACK))
-        w_raw = const.tile([P, PACK, 2 * FEAT], BF16, name="w_raw")
-        nc.scalar.dma_start(
-            out=w_raw[:, :, 0:FEAT], in_=upL_w.rearrange("(p c) n -> p c n", c=PACK)
-        )
-        nc.scalar.dma_start(
-            out=w_raw[:, :, FEAT : 2 * FEAT], in_=upR_w.rearrange("(p c) n -> p c n", c=PACK)
-        )
+        w_raw = []
+        for k, w in enumerate((upL_w, upR_w)):
+            raw = const.tile([P, PACK, FEAT], BF16, name="w_raw%d" % k)
+            nc.scalar.dma_start(out=raw[:], in_=w.rearrange("(p c) n -> p c n", c=PACK))
+            w_raw.append(raw)
         lbias_bf = const.tile([P, 1], BF16, name="lbias_bf")
         nc.scalar.dma_start(out=lbias_bf[:], in_=upL_b.rearrange("(p c) -> p c", c=1))
-        bias_bf = const.tile([P, FEAT], BF16, name="bias_bf")
-        nc.scalar.dma_start(out=bias_bf[:], in_=upR_b.partition_broadcast(P))
-        taps_bf = const.tile([P, TAPS], BF16, name="taps_bf")
-        nc.scalar.dma_start(out=taps_bf[:], in_=conv_w.partition_broadcast(P))
-        cbias_bf = const.tile([P, 1], BF16, name="cbias_bf")
-        nc.scalar.dma_start(out=cbias_bf[:], in_=conv_b.partition_broadcast(P))
+        rbias_bf = const.tile([P, 1], BF16, name="rbias_bf")
+        nc.scalar.dma_start(out=rbias_bf[:], in_=upR_b.rearrange("(p c) -> p c", c=1))
+        conv_bf = const.tile([P, 1], BF16, name="conv_bf")
+        nc.vector.memset(conv_bf[:], 0.0)
+        nc.scalar.dma_start(out=conv_bf[0:TAPS, :], in_=conv_w.rearrange("(p c) -> p c", c=1))
+        nc.scalar.dma_start(
+            out=conv_bf[TAPS : TAPS + 1, :], in_=conv_b.rearrange("(p c) -> p c", c=1)
+        )
         for g in range(1, N_GROUPS):
             load(g)
 
@@ -146,21 +146,32 @@ def tile_mlstmblock_pa_t_kernel(
             normed[g] = t
 
         def norm_constants():
-            cols = const.tile([P, 2 * PACK + 1], F32, name="cols")
+            cols = const.tile([P, 2 * PACK + 3], F32, name="cols")
             nc.vector.tensor_copy(out=cols[:, 0:PACK], in_=lnw_bf[:])
             nc.vector.tensor_copy(out=cols[:, PACK : 2 * PACK], in_=lnb_bf[:])
             nc.vector.tensor_copy(out=cols[:, 2 * PACK : 2 * PACK + 1], in_=lbias_bf[:])
+            nc.vector.tensor_copy(out=cols[:, 2 * PACK + 1 : 2 * PACK + 2], in_=rbias_bf[:])
+            nc.vector.tensor_copy(out=cols[:, 2 * PACK + 2 : 2 * PACK + 3], in_=conv_bf[:])
             return cols
 
         def product_constants():
             w_grouped = const.tile([P, 2 * FEAT, PACK], BF16, name="w_grouped", align_bytes=64)
-            nc.vector.tensor_copy(out=w_grouped[:], in_=w_raw[:].rearrange("p c n -> p n c"))
-            taps = const.tile([P, TAPS], F32, name="taps")
-            nc.vector.tensor_copy(out=taps[:], in_=taps_bf[:])
-            cbias = const.tile([P, 1], F32, name="cbias")
-            nc.vector.tensor_copy(out=cbias[:], in_=cbias_bf[:])
+            for k in range(2):
+                nc.vector.tensor_copy(
+                    out=w_grouped[:, k * FEAT : (k + 1) * FEAT, :],
+                    in_=w_raw[k][:].rearrange("p c n -> p n c"),
+                )
+            spread = psum.tile([P, 2, P], F32, name="spread", tag="cvp")
+            for k in range(2):
+                column = cols[:, 2 * PACK + 1 + k : 2 * PACK + 2 + k]
+                nc.tensor.transpose(
+                    out=spread[:, k, :], in_=column.to_broadcast([P, P]), identity=ident[:]
+                )
             bias_bc = const.tile([P, FEAT], F32, name="bias_bc")
-            nc.vector.tensor_copy(out=bias_bc[:], in_=bias_bf[:])
+            nc.vector.tensor_copy(out=bias_bc[:], in_=spread[:, 0, :])
+            conv_row = const.tile([P, TAPS + 1], F32, name="conv_row")
+            nc.vector.tensor_copy(out=conv_row[:], in_=spread[:, 1, 0 : TAPS + 1])
+            taps, cbias = conv_row[:, 0:TAPS], conv_row[:, TAPS : TAPS + 1]
             w_codes = const.tile([P, 2 * FEAT], U32, name="w_codes", align_bytes=64)
             w_scales = const.tile([P, 2 * FEAT], U8, name="w_scales", align_bytes=64)
             nc.vector.quantize_mx(
@@ -213,14 +224,16 @@ def tile_mlstmblock_pa_t_kernel(
         def regroup(g):
             planes = planes_of.pop(g)
             grp = work.tile([P, GROUP_ROWS, PACK], BF16, name="grp", align_bytes=64)
-            nc.gpsimd.tensor_scalar(
-                out=grp[:],
-                in0=planes[:].rearrange("p c r -> p r c"),
-                scalar1=1.0,
-                scalar2=0.0,
-                op0=ALU.mult,
-                op1=ALU.add,
-            )
+            for j in range(0, SUB, 2):
+                rows = slice(j * P, (j + 2) * P)
+                nc.gpsimd.tensor_scalar(
+                    out=grp[:, rows, :],
+                    in0=planes[:, :, rows].rearrange("p c r -> p r c"),
+                    scalar1=1.0,
+                    scalar2=0.0,
+                    op0=ALU.mult,
+                    op1=ALU.add,
+                )
             grouped[g] = grp
 
         def quantise(g):
@@ -279,7 +292,7 @@ def tile_mlstmblock_pa_t_kernel(
 
         def convolve_on_tensor(g):
             xlt = left_t.pop(g)
-            cvp = psum.tile([P, SUB, FEAT], F32, name="cvp")
+            cvp = psum.tile([P, SUB, FEAT], F32, name="cvp", tag="cvp")
             for j in range(row_tiles_convolved_on_tensor(g)):
                 nc.tensor.matmul(
                     out=cvp[:, j, :],
@@ -300,7 +313,7 @@ def tile_mlstmblock_pa_t_kernel(
                 out=cv[:],
                 in0=left[:, first:, :],
                 scalar1=taps[:, TAPS - 1 : TAPS],
-                scalar2=cbias[:, 0:1],
+                scalar2=cbias,
                 op0=ALU.mult,
                 op1=ALU.add,
             )
@@ -337,7 +350,7 @@ def tile_mlstmblock_pa_t_kernel(
             first = row_tiles_convolved_on_tensor(g)
             xc = work.tile([P, SUB, FEAT], F32, name="xc")
             nc.scalar.activation(
-                out=xc[:, 0:first, :], in_=cvp[:, 0:first, :], func=ACT.Silu, bias=cbias[:, 0:1]
+                out=xc[:, 0:first, :], in_=cvp[:, 0:first, :], func=ACT.Silu, bias=cbias
             )
             if first < SUB:
                 nc.scalar.activation(out=xc[:, first:, :], in_=conv_rest.pop(g)[:], func=ACT.Silu)

@@ -23,7 +23,7 @@ FLOPS = 2 * ROWS * IN * 2 * FEAT
 
 
 def normaliser(nc, g, j):
-    return (nc.vector, nc.vector, nc.scalar, (nc.scalar, nc.gpsimd)[g % 2])[j]
+    return (nc.vector, nc.scalar, nc.scalar, (nc.scalar, nc.gpsimd)[g % 2])[j]
 
 
 def row_tiles_convolved_on_tensor(g):
@@ -39,6 +39,7 @@ def tile_mlstmblock_pa_t_kernel(
         small = ctx.enter_context(tc.tile_pool(name="small", bufs=4))
         work = ctx.enter_context(tc.tile_pool(name="work", bufs=3))
         slots = ctx.enter_context(tc.psum_pool(name="slots", bufs=4))
+        sums = ctx.enter_context(tc.psum_pool(name="sums", bufs=2))
         psum = ctx.enter_context(tc.psum_pool(name="psum", bufs=1))
 
         def group_rows(dram, g):
@@ -95,9 +96,8 @@ def tile_mlstmblock_pa_t_kernel(
         grouped = {}
         mx_words = {}
         left_t_bank = {}
-        right_bank = {}
+        row_banks = {}
         left_t = {}
-        left_bank = {}
         conv_bank = {}
         conv_rest = {}
 
@@ -161,16 +161,18 @@ def tile_mlstmblock_pa_t_kernel(
                     out=w_grouped[:, k * FEAT : (k + 1) * FEAT, :],
                     in_=w_raw[k][:].rearrange("p c n -> p n c"),
                 )
-            spread = psum.tile([P, 2, P], F32, name="spread", tag="cvp")
-            for k in range(2):
-                column = cols[:, 2 * PACK + 1 + k : 2 * PACK + 2 + k]
+            spread = psum.tile([P, 3, P], F32, name="spread", tag="cvp")
+            for k in range(3):
+                column = cols[:, 2 * PACK + k : 2 * PACK + 1 + k]
                 nc.tensor.transpose(
                     out=spread[:, k, :], in_=column.to_broadcast([P, P]), identity=ident[:]
                 )
-            bias_bc = const.tile([P, FEAT], F32, name="bias_bc")
-            nc.vector.tensor_copy(out=bias_bc[:], in_=spread[:, 0, :])
+            bias_bc = const.tile([P, 2 * FEAT], F32, name="bias_bc")
+            nc.vector.tensor_copy(
+                out=bias_bc[:], in_=spread[:, 0:2, :].rearrange("p l n -> p (l n)")
+            )
             conv_row = const.tile([P, TAPS + 1], F32, name="conv_row")
-            nc.vector.tensor_copy(out=conv_row[:], in_=spread[:, 1, 0 : TAPS + 1])
+            nc.vector.tensor_copy(out=conv_row[:], in_=spread[:, 2, 0 : TAPS + 1])
             taps, cbias = conv_row[:, 0:TAPS], conv_row[:, TAPS : TAPS + 1]
             w_codes = const.tile([P, 2 * FEAT], U32, name="w_codes", align_bytes=64)
             w_scales = const.tile([P, 2 * FEAT], U8, name="w_scales", align_bytes=64)
@@ -192,7 +194,25 @@ def tile_mlstmblock_pa_t_kernel(
                     op0=ALU.mult,
                     op1=ALU.add,
                 )
-            return w_codes, w_scales, bias_bc, taps, cbias, band
+            conv_of_bias = const.tile([P, FEAT], F32, name="conv_of_bias")
+            nc.vector.tensor_scalar(
+                out=conv_of_bias[:],
+                in0=bias_bc[:, 0:FEAT],
+                scalar1=taps[:, TAPS - 1 : TAPS],
+                scalar2=cbias,
+                op0=ALU.mult,
+                op1=ALU.add,
+            )
+            for s in range(1, TAPS):
+                nc.vector.scalar_tensor_tensor(
+                    out=conv_of_bias[:, s:FEAT],
+                    in0=bias_bc[:, 0 : FEAT - s],
+                    scalar=taps[:, TAPS - 1 - s : TAPS - s],
+                    in1=conv_of_bias[:, s:FEAT],
+                    op0=ALU.mult,
+                    op1=ALU.add,
+                )
+            return w_codes, w_scales, bias_bc, taps, cbias, band, conv_of_bias
 
         def transpose(g):
             t = normed.pop(g)
@@ -260,19 +280,22 @@ def tile_mlstmblock_pa_t_kernel(
                 stop=True,
             )
             left_t_bank[g] = lt
-            right = psum.tile([P, SUB, FEAT], F32, name="right")
-            for j in range(SUB):
-                sub_cols = slice(j * P, (j + 1) * P)
-                nc.tensor.matmul_mx(
-                    out=right[:, j, :],
-                    lhsT=codes[:, sub_cols].bitcast(FP8X4),
-                    lhsT_scale=scales[:, sub_cols],
-                    rhs=w_codes[:, FEAT : 2 * FEAT].bitcast(FP8X4),
-                    rhs_scale=w_scales[:, FEAT : 2 * FEAT],
-                    start=True,
-                    stop=True,
-                )
-            right_bank[g] = right
+            banks = []
+            for h in range(SUB // 2):
+                acc = sums.tile([P, 2, 2 * FEAT], F32, name="acc")
+                for i in range(2):
+                    sub_cols = slice((2 * h + i) * P, (2 * h + i + 1) * P)
+                    nc.tensor.matmul_mx(
+                        out=acc[:, i, :],
+                        lhsT=codes[:, sub_cols].bitcast(FP8X4),
+                        lhsT_scale=scales[:, sub_cols],
+                        rhs=w_codes[:].bitcast(FP8X4),
+                        rhs_scale=w_scales[:],
+                        start=True,
+                        stop=True,
+                    )
+                banks.append(acc)
+            row_banks[g] = banks
 
         def left_bias(g):
             lt = left_t_bank.pop(g)
@@ -281,14 +304,6 @@ def tile_mlstmblock_pa_t_kernel(
                 out=xlt[:], in_=lt[:], func=ACT.Identity, bias=cols[:, 2 * PACK : 2 * PACK + 1]
             )
             left_t[g] = xlt
-
-        def left_rows(g):
-            left = psum.tile([P, SUB, FEAT], F32, name="left")
-            for j in range(SUB):
-                nc.tensor.transpose(
-                    out=left[:, j, :], in_=left_t[g][:, j * P : (j + 1) * P], identity=ident[:]
-                )
-            left_bank[g] = left
 
         def convolve_on_tensor(g):
             xlt = left_t.pop(g)
@@ -304,46 +319,37 @@ def tile_mlstmblock_pa_t_kernel(
             conv_bank[g] = cvp
 
         def convolve_on_vector(g):
-            left = left_bank[g]
             first = row_tiles_convolved_on_tensor(g)
             if first == SUB:
                 return
             cv = work.tile([P, SUB - first, FEAT], F32, name="cv")
-            nc.vector.tensor_scalar(
-                out=cv[:],
-                in0=left[:, first:, :],
-                scalar1=taps[:, TAPS - 1 : TAPS],
-                scalar2=cbias,
-                op0=ALU.mult,
-                op1=ALU.add,
-            )
-            for s in range(1, TAPS):
+            for s in range(TAPS):
                 nc.vector.scalar_tensor_tensor(
                     out=cv[:, :, s:FEAT],
-                    in0=left[:, first:, 0 : FEAT - s],
+                    in0=row_banks[g][1][:, :, 0 : FEAT - s],
                     scalar=taps[:, TAPS - 1 - s : TAPS - s],
-                    in1=cv[:, :, s:FEAT],
+                    in1=cv[:, :, s:FEAT]
+                    if s > 0
+                    else conv_of_bias[:].unsqueeze(1).to_broadcast([P, SUB - first, FEAT]),
                     op0=ALU.mult,
                     op1=ALU.add,
                 )
             conv_rest[g] = cv
 
-        def left_out(g):
-            left = left_bank[g]
-            o_left = work.tile([P, SUB, FEAT], F32, name="o_left")
-            nc.scalar.copy(out=o_left[:], in_=left[:])
-            nc.sync.dma_start(out=group_rows(out_0, g), in_=o_left[:])
-
-        def right_out(g):
-            right = right_bank.pop(g)
-            o_right = work.tile([P, SUB, FEAT], F32, name="o_right")
-            nc.vector.tensor_tensor(
-                out=o_right[:],
-                in0=right[:],
-                in1=bias_bc[:].unsqueeze(1).to_broadcast([P, SUB, FEAT]),
-                op=ALU.add,
-            )
-            nc.sync.dma_start(out=group_rows(out_2, g), in_=o_right[:])
+        def add_bias(g):
+            o = work.tile([P, 2, SUB, FEAT], F32, name="o")
+            for h, acc in enumerate(row_banks.pop(g)):
+                nc.vector.tensor_tensor(
+                    out=o[:, :, 2 * h : 2 * h + 2, :].rearrange("p l j n -> p j l n"),
+                    in0=acc[:].rearrange("p j (l n) -> p j l n", l=2),
+                    in1=bias_bc[:]
+                    .rearrange("p (l n) -> p l n", l=2)
+                    .unsqueeze(1)
+                    .to_broadcast([P, 2, 2, FEAT]),
+                    op=ALU.add,
+                )
+            nc.sync.dma_start(out=group_rows(out_0, g), in_=o[:, 0, :, :])
+            nc.sync.dma_start(out=group_rows(out_2, g), in_=o[:, 1, :, :])
 
         def silu(g):
             cvp = conv_bank.pop(g)
@@ -358,7 +364,7 @@ def tile_mlstmblock_pa_t_kernel(
 
         stats(0)
         cols = norm_constants()
-        w_codes, w_scales, bias_bc, taps, cbias, band = product_constants()
+        w_codes, w_scales, bias_bc, taps, cbias, band, conv_of_bias = product_constants()
         with tc.high_priority(offset=1000):
             normalise(0)
         for g in range(N_GROUPS):
@@ -371,9 +377,7 @@ def tile_mlstmblock_pa_t_kernel(
             quantise(g)
             project(g)
             left_bias(g)
-            left_rows(g)
             convolve_on_tensor(g)
-            left_out(g)
-            right_out(g)
             convolve_on_vector(g)
+            add_bias(g)
             silu(g)

from contextlib import ExitStack

import concourse.mybir as mybir
from concourse.masks import make_identity

F32 = mybir.dt.float32
BF16 = mybir.dt.bfloat16
U32 = mybir.dt.uint32
U8 = mybir.dt.uint8
FP8X4 = mybir.dt.float8_e4m3fn_x4
ALU = mybir.AluOpType
ACT = mybir.ActivationFunctionType

P = 128
PACK = 4
ROWS, IN, FEAT, TAPS = 8192, 512, 128, 4
EPS = 1e-5
SUB = 4
GROUP_ROWS = P * SUB
N_GROUPS = ROWS // GROUP_ROWS

FLOPS = 2 * ROWS * IN * 2 * FEAT


def normaliser(nc, g, j):
    return (nc.vector, nc.scalar, nc.scalar, (nc.scalar, nc.gpsimd)[g % 2])[j]


def row_tiles_convolved_on_tensor(g):
    return SUB // 2 if g % 2 == 1 and g < N_GROUPS - 1 else SUB


def tile_mlstmblock_pa_t_kernel(
    tc, x, ln_w, ln_b, upL_w, upL_b, upR_w, upR_b, conv_w, conv_b, out_0, out_1, out_2
):
    nc = tc.nc
    with ExitStack() as ctx:
        const = ctx.enter_context(tc.tile_pool(name="const", bufs=1))
        small = ctx.enter_context(tc.tile_pool(name="small", bufs=4))
        work = ctx.enter_context(tc.tile_pool(name="work", bufs=3))
        slots = ctx.enter_context(tc.psum_pool(name="slots", bufs=4))
        sums = ctx.enter_context(tc.psum_pool(name="sums", bufs=2))
        psum = ctx.enter_context(tc.psum_pool(name="psum", bufs=1))

        def group_rows(dram, g):
            return dram[g * GROUP_ROWS : (g + 1) * GROUP_ROWS, :].rearrange(
                "(p j) n -> p j n", j=SUB
            )

        x_sb = [const.tile([P, SUB, IN], BF16, name="x%d" % g) for g in range(N_GROUPS)]

        def load(g):
            nc.sync.dma_start(out=x_sb[g][:], in_=group_rows(x, g))

        load(0)
        lnw_bf = const.tile([P, PACK], BF16, name="lnw_bf")
        nc.scalar.dma_start(out=lnw_bf[:], in_=ln_w.rearrange("(p c) -> p c", c=PACK))
        lnb_bf = const.tile([P, PACK], BF16, name="lnb_bf")
        nc.scalar.dma_start(out=lnb_bf[:], in_=ln_b.rearrange("(p c) -> p c", c=PACK))
        w_raw = []
        for k, w in enumerate((upL_w, upR_w)):
            raw = const.tile([P, PACK, FEAT], BF16, name="w_raw%d" % k)
            nc.scalar.dma_start(out=raw[:], in_=w.rearrange("(p c) n -> p c n", c=PACK))
            w_raw.append(raw)
        lbias_bf = const.tile([P, 1], BF16, name="lbias_bf")
        nc.scalar.dma_start(out=lbias_bf[:], in_=upL_b.rearrange("(p c) -> p c", c=1))
        rbias_bf = const.tile([P, 1], BF16, name="rbias_bf")
        nc.scalar.dma_start(out=rbias_bf[:], in_=upR_b.rearrange("(p c) -> p c", c=1))
        conv_bf = const.tile([P, 1], BF16, name="conv_bf")
        nc.vector.memset(conv_bf[:], 0.0)
        nc.scalar.dma_start(out=conv_bf[0:TAPS, :], in_=conv_w.rearrange("(p c) -> p c", c=1))
        nc.scalar.dma_start(
            out=conv_bf[TAPS : TAPS + 1, :], in_=conv_b.rearrange("(p c) -> p c", c=1)
        )
        for g in range(1, N_GROUPS):
            load(g)

        neg_half = const.tile([P, SUB], F32, name="neg_half")
        nc.gpsimd.memset(neg_half[:], -0.5)
        ident = const.tile([P, P], F32, name="ident")
        make_identity(nc, ident[:])
        first_silu = const.tile([P, 1], F32, name="first_silu")
        nc.scalar.activation(out=first_silu[:], in_=neg_half[:, 0:1], func=ACT.Silu)

        row_stats = []
        for k in range(2):
            st = const.tile([P, SUB, 9], F32, name="st%d" % k)
            nc.vector.memset(st[:], 0.0)
            nc.vector.memset(st[:, :, 8], IN * EPS)
            row_stats.append(st)

        mean_var = {}
        normed = {}
        t_banks = {}
        planes_of = {}
        grouped = {}
        mx_words = {}
        left_t_bank = {}
        row_banks = {}
        left_t = {}
        conv_bank = {}
        conv_rest = {}

        def stats(g):
            st = row_stats[g % 2]
            mv = small.tile([P, SUB, 2], F32, name="mv")
            for j in range(SUB):
                nc.vector.bn_stats(out=st[:, j, 0:6], in_=x_sb[g][:, j, :])
            neg_mean = small.tile([P, SUB], F32, name="neg_mean")
            with tc.high_priority(offset=1000):
                for j in range(SUB):
                    nc.vector.bn_aggr(out=mv[:, j, :], in_=st[:, j, :])
                nc.vector.tensor_scalar(
                    out=neg_mean[:], in0=mv[:, :, 0], scalar1=-1.0, scalar2=None, op0=ALU.mult
                )
            mean_var[g] = (neg_mean, mv)

        def normalise(g):
            neg_mean, mv = mean_var.pop(g)
            rstd = small.tile([P, SUB], F32, name="rstd")
            nc.gpsimd.tensor_tensor(out=rstd[:], in0=mv[:, :, 1], in1=neg_half[:], op=ALU.pow)
            shift = small.tile([P, SUB], F32, name="shift")
            nc.gpsimd.tensor_tensor(out=shift[:], in0=neg_mean[:], in1=rstd[:], op=ALU.mult)
            t = work.tile([P, SUB, IN], F32, name="t")
            for j in range(SUB):
                t_j = t[:, j, :].rearrange("p (c m) -> p c m", c=PACK)
                x_j = x_sb[g][:, j, :].rearrange("p (m c) -> p c m", c=PACK)
                engine = normaliser(nc, g, j)
                if engine != nc.scalar:
                    engine.tensor_scalar(
                        out=t_j,
                        in0=x_j,
                        scalar1=neg_mean[:, j : j + 1],
                        scalar2=rstd[:, j : j + 1],
                        op0=ALU.add,
                        op1=ALU.mult,
                    )
                else:
                    nc.scalar.activation(
                        out=t_j,
                        in_=x_j,
                        func=ACT.Identity,
                        scale=rstd[:, j : j + 1],
                        bias=shift[:, j : j + 1],
                    )
            normed[g] = t

        def norm_constants():
            cols = const.tile([P, 2 * PACK + 3], F32, name="cols")
            nc.vector.tensor_copy(out=cols[:, 0:PACK], in_=lnw_bf[:])
            nc.vector.tensor_copy(out=cols[:, PACK : 2 * PACK], in_=lnb_bf[:])
            nc.vector.tensor_copy(out=cols[:, 2 * PACK : 2 * PACK + 1], in_=lbias_bf[:])
            nc.vector.tensor_copy(out=cols[:, 2 * PACK + 1 : 2 * PACK + 2], in_=rbias_bf[:])
            nc.vector.tensor_copy(out=cols[:, 2 * PACK + 2 : 2 * PACK + 3], in_=conv_bf[:])
            return cols

        def product_constants():
            w_grouped = const.tile([P, 2 * FEAT, PACK], BF16, name="w_grouped", align_bytes=64)
            for k in range(2):
                nc.vector.tensor_copy(
                    out=w_grouped[:, k * FEAT : (k + 1) * FEAT, :],
                    in_=w_raw[k][:].rearrange("p c n -> p n c"),
                )
            spread = psum.tile([P, 3, P], F32, name="spread", tag="cvp")
            for k in range(3):
                column = cols[:, 2 * PACK + k : 2 * PACK + 1 + k]
                nc.tensor.transpose(
                    out=spread[:, k, :], in_=column.to_broadcast([P, P]), identity=ident[:]
                )
            bias_bc = const.tile([P, 2 * FEAT], F32, name="bias_bc")
            nc.vector.tensor_copy(
                out=bias_bc[:], in_=spread[:, 0:2, :].rearrange("p l n -> p (l n)")
            )
            conv_row = const.tile([P, TAPS + 1], F32, name="conv_row")
            nc.vector.tensor_copy(out=conv_row[:], in_=spread[:, 2, 0 : TAPS + 1])
            taps, cbias = conv_row[:, 0:TAPS], conv_row[:, TAPS : TAPS + 1]
            w_codes = const.tile([P, 2 * FEAT], U32, name="w_codes", align_bytes=64)
            w_scales = const.tile([P, 2 * FEAT], U8, name="w_scales", align_bytes=64)
            nc.vector.quantize_mx(
                out=w_codes[:].bitcast(FP8X4),
                scales=w_scales[:],
                in_=w_grouped[:].rearrange("p n c -> p (n c)"),
            )
            band = const.tile([P, FEAT], F32, name="band")
            nc.vector.tensor_scalar(
                out=band[:], in0=ident[:], scalar1=taps[:, TAPS - 1 : TAPS], scalar2=None, op0=ALU.mult
            )
            for s in range(1, TAPS):
                nc.vector.scalar_tensor_tensor(
                    out=band[:, s:FEAT],
                    in0=ident[:, 0 : FEAT - s],
                    scalar=taps[:, TAPS - 1 - s : TAPS - s],
                    in1=band[:, s:FEAT],
                    op0=ALU.mult,
                    op1=ALU.add,
                )
            conv_of_bias = const.tile([P, FEAT], F32, name="conv_of_bias")
            nc.vector.tensor_scalar(
                out=conv_of_bias[:],
                in0=bias_bc[:, 0:FEAT],
                scalar1=taps[:, TAPS - 1 : TAPS],
                scalar2=cbias,
                op0=ALU.mult,
                op1=ALU.add,
            )
            for s in range(1, TAPS):
                nc.vector.scalar_tensor_tensor(
                    out=conv_of_bias[:, s:FEAT],
                    in0=bias_bc[:, 0 : FEAT - s],
                    scalar=taps[:, TAPS - 1 - s : TAPS - s],
                    in1=conv_of_bias[:, s:FEAT],
                    op0=ALU.mult,
                    op1=ALU.add,
                )
            return w_codes, w_scales, bias_bc, taps, cbias, band, conv_of_bias

        def transpose(g):
            t = normed.pop(g)
            banks = []
            for c in range(PACK):
                bank = slots.tile([P, GROUP_ROWS], F32, name="bank")
                for j in range(SUB):
                    nc.tensor.transpose(
                        out=bank[:, j * P : (j + 1) * P],
                        in_=t[:, j, c * P : (c + 1) * P],
                        identity=ident[:],
                    )
                banks.append(bank)
            t_banks[g] = banks

        def scale_shift(g):
            banks = t_banks.pop(g)
            planes = work.tile([P, PACK, GROUP_ROWS], BF16, name="planes")
            for c in range(PACK):
                nc.scalar.activation(
                    out=planes[:, c, :],
                    in_=banks[c][:],
                    func=ACT.Identity,
                    scale=cols[:, c : c + 1],
                    bias=cols[:, PACK + c : PACK + c + 1],
                )
            planes_of[g] = planes

        def regroup(g):
            planes = planes_of.pop(g)
            grp = work.tile([P, GROUP_ROWS, PACK], BF16, name="grp", align_bytes=64)
            for j in range(0, SUB, 2):
                rows = slice(j * P, (j + 2) * P)
                nc.gpsimd.tensor_scalar(
                    out=grp[:, rows, :],
                    in0=planes[:, :, rows].rearrange("p c r -> p r c"),
                    scalar1=1.0,
                    scalar2=0.0,
                    op0=ALU.mult,
                    op1=ALU.add,
                )
            grouped[g] = grp

        def quantise(g):
            grp = grouped.pop(g)
            codes = work.tile([P, GROUP_ROWS], U32, name="codes", align_bytes=64)
            scales = work.tile([P, GROUP_ROWS], U8, name="scales", align_bytes=64)
            nc.vector.quantize_mx(
                out=codes[:].bitcast(FP8X4),
                scales=scales[:],
                in_=grp[:].rearrange("p r c -> p (r c)"),
            )
            mx_words[g] = (codes, scales)

        def project(g):
            codes, scales = mx_words.pop(g)
            lt = psum.tile([P, GROUP_ROWS], F32, name="lt")
            nc.tensor.matmul_mx(
                out=lt[:],
                lhsT=w_codes[:, 0:FEAT].bitcast(FP8X4),
                lhsT_scale=w_scales[:, 0:FEAT],
                rhs=codes[:].bitcast(FP8X4),
                rhs_scale=scales[:],
                start=True,
                stop=True,
            )
            left_t_bank[g] = lt
            banks = []
            for h in range(SUB // 2):
                acc = sums.tile([P, 2, 2 * FEAT], F32, name="acc")
                for i in range(2):
                    sub_cols = slice((2 * h + i) * P, (2 * h + i + 1) * P)
                    nc.tensor.matmul_mx(
                        out=acc[:, i, :],
                        lhsT=codes[:, sub_cols].bitcast(FP8X4),
                        lhsT_scale=scales[:, sub_cols],
                        rhs=w_codes[:].bitcast(FP8X4),
                        rhs_scale=w_scales[:],
                        start=True,
                        stop=True,
                    )
                banks.append(acc)
            row_banks[g] = banks

        def left_bias(g):
            lt = left_t_bank.pop(g)
            xlt = work.tile([P, GROUP_ROWS], F32, name="xlt")
            nc.scalar.activation(
                out=xlt[:], in_=lt[:], func=ACT.Identity, bias=cols[:, 2 * PACK : 2 * PACK + 1]
            )
            left_t[g] = xlt

        def convolve_on_tensor(g):
            xlt = left_t.pop(g)
            cvp = psum.tile([P, SUB, FEAT], F32, name="cvp", tag="cvp")
            for j in range(row_tiles_convolved_on_tensor(g)):
                nc.tensor.matmul(
                    out=cvp[:, j, :],
                    lhsT=xlt[:, j * P : (j + 1) * P],
                    rhs=band[:],
                    start=True,
                    stop=True,
                )
            conv_bank[g] = cvp

        def convolve_on_vector(g):
            first = row_tiles_convolved_on_tensor(g)
            if first == SUB:
                return
            cv = work.tile([P, SUB - first, FEAT], F32, name="cv")
            for s in range(TAPS):
                nc.vector.scalar_tensor_tensor(
                    out=cv[:, :, s:FEAT],
                    in0=row_banks[g][1][:, :, 0 : FEAT - s],
                    scalar=taps[:, TAPS - 1 - s : TAPS - s],
                    in1=cv[:, :, s:FEAT]
                    if s > 0
                    else conv_of_bias[:].unsqueeze(1).to_broadcast([P, SUB - first, FEAT]),
                    op0=ALU.mult,
                    op1=ALU.add,
                )
            conv_rest[g] = cv

        def add_bias(g):
            o = work.tile([P, 2, SUB, FEAT], F32, name="o")
            for h, acc in enumerate(row_banks.pop(g)):
                nc.vector.tensor_tensor(
                    out=o[:, :, 2 * h : 2 * h + 2, :].rearrange("p l j n -> p j l n"),
                    in0=acc[:].rearrange("p j (l n) -> p j l n", l=2),
                    in1=bias_bc[:]
                    .rearrange("p (l n) -> p l n", l=2)
                    .unsqueeze(1)
                    .to_broadcast([P, 2, 2, FEAT]),
                    op=ALU.add,
                )
            nc.sync.dma_start(out=group_rows(out_0, g), in_=o[:, 0, :, :])
            nc.sync.dma_start(out=group_rows(out_2, g), in_=o[:, 1, :, :])

        def silu(g):
            cvp = conv_bank.pop(g)
            first = row_tiles_convolved_on_tensor(g)
            xc = work.tile([P, SUB, FEAT], F32, name="xc")
            nc.scalar.activation(
                out=xc[:, 0:first, :], in_=cvp[:, 0:first, :], func=ACT.Silu, bias=cbias
            )
            if first < SUB:
                nc.scalar.activation(out=xc[:, first:, :], in_=conv_rest.pop(g)[:], func=ACT.Silu)
            nc.sync.dma_start(out=group_rows(out_1, g), in_=xc[:])

        stats(0)
        cols = norm_constants()
        w_codes, w_scales, bias_bc, taps, cbias, band, conv_of_bias = product_constants()
        with tc.high_priority(offset=1000):
            normalise(0)
        for g in range(N_GROUPS):
            if g + 1 < N_GROUPS:
                stats(g + 1)
                normalise(g + 1)
            transpose(g)
            scale_shift(g)
            regroup(g)
            quantise(g)
            project(g)
            left_bias(g)
            convolve_on_tensor(g)
            convolve_on_vector(g)
            add_bias(g)
            silu(g)
